import numpy as np
import ml_dtypes


def mxq(x, axis, fmt="e4m3"):
    dtype, down = {"e4m3": (ml_dtypes.float8_e4m3fn, 7), "e5m2": (ml_dtypes.float8_e5m2, 14)}[fmt]
    v = np.moveaxis(np.asarray(x, np.float32).astype(ml_dtypes.bfloat16).astype(np.float64), axis, -1)
    blocks = v.reshape(v.shape[:-1] + (-1, 32))
    amax = np.abs(blocks).max(-1, keepdims=True)
    byte = np.maximum(np.where(amax > 0, np.frexp(amax)[1] - 1 + 127, 0) - down, 1)
    scale = np.exp2(byte - 127.0)
    codes = (blocks / scale).astype(np.float32).astype(dtype).astype(np.float64)
    return np.moveaxis((codes * scale).reshape(v.shape), -1, axis)


WIDE = False


def mx_kscale(k):
    if not WIDE:
        return np.ones(k)
    levels = np.array([10, -10, 5, -5, 0])
    a = np.random.permutation(np.resize(levels, k // 512 * 4)).reshape(k // 512, 4)
    idx = np.arange(k)
    return np.exp2(a[idx // 512, idx % 128 // 32])


BF16 = ml_dtypes.bfloat16


def bf(x):
    return np.asarray(x, np.float32).astype(BF16)


def f64(x):
    return np.asarray(x).astype(np.float64)


E2M1 = np.array([0.0, 0.5, 1.0, 1.5, 2.0, 3.0, 4.0, 6.0, -0.0, -0.5, -1.0, -1.5, -2.0, -3.0, -4.0, -6.0])


def pack_weight(w, fmt):
    k, n = w.shape
    w = f64(bf(w)).reshape(k // 32, 32, n)
    amax = np.abs(w).max(1)
    if fmt == "e4m3":
        byte = np.frexp(amax)[1] - 1 + 127 - 7
    else:
        mant, ex = np.frexp(amax / 6.0)
        byte = np.where(mant > 0.5, ex, ex - 1) + 127
    byte = np.clip(np.where(amax > 0, byte, 1), 1, 254)
    scaled = (w * np.exp2(127.0 - byte)[:, None, :]).reshape(k, n).astype(np.float32)
    by_word = np.ascontiguousarray(scaled.reshape(k // 512, 128, 4, n).transpose(0, 1, 3, 2))
    if fmt == "e4m3":
        words = by_word.astype(ml_dtypes.float8_e4m3fn).view(np.uint8)
    else:
        c = by_word.astype(ml_dtypes.float4_e2m1fn).view(np.uint8) & 0xF
        words = c[..., 0::2] | (c[..., 1::2] << 4)
    return np.ascontiguousarray(words), np.ascontiguousarray(byte.astype(np.uint8).reshape(k // 512, 16, n))


def unpack_weight(words, scales, fmt):
    g, p, n, _ = words.shape
    if fmt == "e4m3":
        vals = np.ascontiguousarray(words).view(ml_dtypes.float8_e4m3fn).astype(np.float64)
    else:
        nib = np.empty((g, p, n, 4), np.uint8)
        nib[..., 0::2] = words & 0xF
        nib[..., 1::2] = words >> 4
        vals = E2M1[nib]
    vals = vals * np.repeat(np.exp2(scales.astype(np.float64) - 127.0), 8, axis=1)[..., None]
    return vals.transpose(0, 1, 3, 2).reshape(g * 512, n)


B, C, HH, WW = 4, 1024, 16, 16
P = HH * WW
EPS = 1e-05
FMT = "e4m3"


def setup_inputs():
    s = mx_kscale(C)
    lev = np.random.uniform(0.5, 1.5, (B, C, 1, 1))
    x = (lev + 0.8 * np.random.standard_normal((B, C, HH, WW))) * s[None, :, None, None]
    r = s[:, None] / s[None, :]
    Wc = np.random.standard_normal((C, C)) * 0.7 / np.sqrt(C) * r
    bc = bf(np.random.standard_normal(C) * 0.3 * s)
    W1 = np.random.standard_normal((C, C)) * 1.4 / np.sqrt(C) * r
    b1 = bf(np.random.standard_normal(C) * 0.5 * s)
    Wc_words, Wc_scales = pack_weight(np.ascontiguousarray(Wc.T), FMT)
    W1_words, W1_scales = pack_weight(np.ascontiguousarray(W1.T), FMT)
    return {"x": bf(x),
            "Wc_words": Wc_words, "Wc_scales": Wc_scales, "bc": bc,
            "W1_words": W1_words, "W1_scales": W1_scales, "b1": b1}


def reference(x, Wc_words, Wc_scales, bc, W1_words, W1_scales, b1):
    x = f64(x)
    out1 = x.mean(axis=(2, 3), keepdims=True)
    out3 = x.max(axis=(2, 3), keepdims=True)
    xq = mxq(x, 1, "e4m3").reshape(B, C, P)
    out2 = ((unpack_weight(Wc_words, Wc_scales, FMT).T @ xq) + f64(bc)[None, :, None]).reshape(B, C, HH, WW)
    out4 = ((unpack_weight(W1_words, W1_scales, FMT).T @ xq) + f64(b1)[None, :, None]).reshape(B, C, HH, WW)
    return out2 / (out1 + EPS), out4 / (out3 + EPS)

@@ -1,0 +1,239 @@
+from contextlib import ExitStack
+
+import concourse.mybir as mybir
+from concourse.masks import make_identity
+
+F32 = mybir.dt.float32
+BF16 = mybir.dt.bfloat16
+I32 = mybir.dt.int32
+U32 = mybir.dt.uint32
+U8 = mybir.dt.uint8
+FP8X4 = mybir.dt.float8_e4m3fn_x4
+ALU = mybir.AluOpType
+ACT = mybir.ActivationFunctionType
+AX = mybir.AxisListType
+
+IMAGES = 4
+CHANNELS = 1024
+PIXELS = 256
+EPS = 1e-05
+
+P = 128
+PACK = 4
+PASSES = CHANNELS // (P * PACK)
+ROWS = PASSES * PACK
+O_TILES = CHANNELS // P
+QUADRANTS = 4
+IN_QUADRANT = P // QUADRANTS
+SUM_CHUNK = 16
+BANK_TILES = 2
+STORE_TILES = 4
+MAX_HALVINGS = 3
+VECTOR_EVERY = 4
+
+FLOPS = 2 * 2 * CHANNELS * CHANNELS * IMAGES * PIXELS
+
+
+def tile_wb_pa_kernel(tc, x, Wc_words, Wc_scales, bc, W1_words, W1_scales, b1, out_0, out_1):
+    nc = tc.nc
+    words_in = (Wc_words, W1_words)
+    scales_in = (Wc_scales, W1_scales)
+    bias_in = (bc, b1)
+    outs = (out_0, out_1)
+
+    with ExitStack() as ctx:
+        const = ctx.enter_context(tc.tile_pool(name="const", bufs=1))
+        image = ctx.enter_context(tc.tile_pool(name="image", bufs=1))
+        result = ctx.enter_context(tc.tile_pool(name="result", bufs=1))
+        acc_psum = ctx.enter_context(tc.psum_pool(name="acc_psum", bufs=4))
+        sum_psum = ctx.enter_context(tc.psum_pool(name="sum_psum", bufs=2))
+        small_psum = ctx.enter_context(tc.psum_pool(name="small_psum", bufs=1))
+
+        w_planes = const.tile([P, CHANNELS], U8, align_bytes=64)
+        nc.vector.memset(w_planes[:].bitcast(I32), 0)
+        bias_rows = const.tile([P, P], BF16)
+        nc.vector.memset(bias_rows[:], 0.0)
+
+        x_sb = []
+        for b in range(IMAGES):
+            x_b = image.tile([P, ROWS, PIXELS], BF16, name="x%d" % b)
+            nc.sync.dma_start(
+                out=x_b[:].rearrange("p (g t) n -> p g (t n)", g=PASSES),
+                in_=x[b].rearrange("(g p t) h w -> p g (t h w)", g=PASSES, p=P, t=PACK),
+            )
+            x_sb.append(x_b)
+
+        w_words = []
+        for w in range(2):
+            for quadrant in range(QUADRANTS):
+                first = IN_QUADRANT * quadrant + PACK * PASSES * w
+                nc.sync.dma_start(
+                    out=w_planes[first : first + PACK * PASSES, :].bitcast(I32),
+                    in_=scales_in[w][:, PACK * quadrant : PACK * (quadrant + 1), :].bitcast(I32),
+                )
+            words = const.tile([P, PASSES, CHANNELS], I32, name="words%d" % w, align_bytes=64)
+            nc.sync.dma_start(out=words[:], in_=words_in[w].rearrange("g p n t -> p g (n t)").bitcast(I32))
+            w_words.append(words)
+
+        ident_bf = const.tile([P, P], BF16)
+        make_identity(nc, ident_bf[:])
+        ident = const.tile([P, P], F32)
+        make_identity(nc, ident[:])
+        for w in range(2):
+            nc.gpsimd.dma_start(
+                out=bias_rows[O_TILES * w : O_TILES * (w + 1), :],
+                in_=bias_in[w].rearrange("(j m) -> j m", m=P),
+            )
+
+        same_r = const.tile([P, IN_QUADRANT], F32)
+        nc.vector.tensor_reduce(
+            out=same_r[:], in_=ident[:].rearrange("p (q r) -> p r q", q=QUADRANTS), axis=AX.X, op=ALU.add
+        )
+        spread = const.tile([P, PACK, IN_QUADRANT, PACK], F32)
+        nc.vector.memset(spread[:], 0.0)
+        for t in range(PACK):
+            nc.vector.tensor_copy(out=spread[:, t, :, t : t + 1], in_=same_r[:].unsqueeze(2))
+        same_q = const.tile([P, QUADRANTS], F32)
+        nc.vector.tensor_reduce(
+            out=same_q[:], in_=ident[:].rearrange("p (q r) -> p q r", q=QUADRANTS), axis=AX.X, op=ALU.add
+        )
+        pick = const.tile([P, QUADRANTS, 2], F32)
+        nc.vector.tensor_scalar(
+            out=pick[:, :, 0:1], in0=same_q[:].unsqueeze(2), scalar1=1.0 / PIXELS, scalar2=None, op0=ALU.mult
+        )
+        nc.vector.tensor_copy(out=pick[:, :, 1:2], in_=same_q[:].unsqueeze(2))
+
+        bias_t = small_psum.tile([P, P], BF16)
+        nc.tensor.transpose(bias_t[:], bias_rows[:], ident_bf[:])
+        bias = const.tile([P, 2, O_TILES], F32)
+        nc.vector.tensor_copy(out=bias[:].rearrange("p w j -> p (w j)"), in_=bias_t[:, 0 : 2 * O_TILES])
+
+        x_codes = []
+        x_planes = []
+        inverse = []
+        offset = []
+
+        def prepare(b):
+            x_b = x_sb[b]
+            stat = image.tile([P, 2, ROWS], F32, name="stat%d" % b)
+
+            sums = sum_psum.tile([P, ROWS, SUM_CHUNK], F32, name="sums")
+            chunks = PIXELS // SUM_CHUNK
+            for c in range(chunks):
+                nc.tensor.matmul(
+                    out=sums[:],
+                    lhsT=ident_bf[:],
+                    rhs=x_b[:, :, SUM_CHUNK * c : SUM_CHUNK * (c + 1)],
+                    start=(c == 0),
+                    stop=(c == chunks - 1),
+                )
+            nc.vector.tensor_reduce(out=stat[:, 0, :], in_=sums[:], axis=AX.X, op=ALU.add)
+
+            widest = x_b
+            for halving in range(1, MAX_HALVINGS + 1):
+                width = PIXELS >> halving
+                narrower = image.tile([P, ROWS, width], BF16, name="max%d_%d" % (b, width))
+                nc.vector.tensor_tensor(
+                    out=narrower[:], in0=widest[:, :, 0:width], in1=widest[:, :, width : 2 * width], op=ALU.max
+                )
+                widest = narrower
+            nc.vector.tensor_reduce(out=stat[:, 1, :], in_=widest[:], axis=AX.X, op=ALU.max)
+
+            masked = image.tile([P, QUADRANTS * 2 * PASSES, PACK], F32, name="masked%d" % b)
+            shape = [P, QUADRANTS, 2, ROWS]
+            nc.vector.tensor_tensor(
+                out=masked[:].rearrange("p (q s g) t -> p q s (g t)", q=QUADRANTS, s=2),
+                in0=stat[:].unsqueeze(1).to_broadcast(shape),
+                in1=pick[:].unsqueeze(3).to_broadcast(shape),
+                op=ALU.mult,
+            )
+            moved = small_psum.tile([P, QUADRANTS * 2 * PASSES], F32, name="moved")
+            for t in range(PACK):
+                nc.tensor.matmul(
+                    out=moved[:],
+                    lhsT=spread[:, t].rearrange("p r u -> p (r u)"),
+                    rhs=masked[:, :, t],
+                    start=(t == 0),
+                    stop=(t == PACK - 1),
+                )
+
+            grouped = image.tile([P, PASSES, PIXELS, PACK], BF16, name="grouped%d" % b, align_bytes=64)
+            for g in range(PASSES):
+                nc.vector.tensor_copy(
+                    out=grouped[:, g].rearrange("p (c i) t -> p c t i", i=4),
+                    in_=x_b[:, PACK * g : PACK * (g + 1), :].rearrange("p t (c i) -> p c t i", i=4),
+                )
+            codes = image.tile([P, PASSES * PIXELS], U32, name="codes%d" % b, align_bytes=64)
+            plane = image.tile([P, PASSES * PIXELS], U8, name="plane%d" % b, align_bytes=64)
+            nc.vector.quantize_mx(
+                out=codes[:].bitcast(FP8X4),
+                scales=plane[:],
+                in_=grouped[:].rearrange("p g n t -> p (g n t)"),
+            )
+            x_codes.append(codes)
+            x_planes.append(plane)
+
+            divisor = image.tile([P, 2, O_TILES], F32, name="divisor%d" % b)
+            nc.vector.tensor_scalar(
+                out=divisor[:].rearrange("p s (g q) -> p q s g", q=QUADRANTS),
+                in0=moved[:].rearrange("p (q s g) -> p q s g", q=QUADRANTS, s=2),
+                scalar1=EPS,
+                scalar2=None,
+                op0=ALU.add,
+            )
+            inverse_b = image.tile([P, 2, O_TILES], F32, name="inverse%d" % b)
+            nc.vector.reciprocal(out=inverse_b[:], in_=divisor[:])
+            offset_b = image.tile([P, 2, O_TILES], F32, name="offset%d" % b)
+            nc.vector.tensor_tensor(out=offset_b[:], in0=bias[:], in1=inverse_b[:], op=ALU.mult)
+            inverse.append(inverse_b)
+            offset.append(offset_b)
+
+        def convolve(b, w):
+            y = result.tile([P, O_TILES, PIXELS], F32, name="y%d_%d" % (b, w))
+            out_view = outs[w][b].rearrange("(j m) h w -> m j (h w)", m=P)
+            for bank in range(O_TILES // BANK_TILES):
+                acc = acc_psum.tile([P, BANK_TILES, PIXELS], F32, name="acc")
+                for h in range(BANK_TILES):
+                    j = BANK_TILES * bank + h
+                    for g in range(PASSES):
+                        nc.tensor.matmul_mx(
+                            out=acc[:, h, :],
+                            lhsT=w_words[w][:, g, P * j : P * (j + 1)].bitcast(FP8X4),
+                            lhsT_scale=w_planes[PACK * (PASSES * w + g) : P, P * j : P * (j + 1)],
+                            rhs=x_codes[b][:, PIXELS * g : PIXELS * (g + 1)].bitcast(FP8X4),
+                            rhs_scale=x_planes[b][:, PIXELS * g : PIXELS * (g + 1)],
+                            start=(g == 0),
+                            stop=(g == PASSES - 1),
+                        )
+                for h in range(BANK_TILES):
+                    j = BANK_TILES * bank + h
+                    if bank % VECTOR_EVERY == VECTOR_EVERY - 1:
+                        nc.vector.tensor_scalar(
+                            out=y[:, j, :],
+                            in0=acc[:, h, :],
+                            scalar1=inverse[b][:, w, j : j + 1],
+                            scalar2=offset[b][:, w, j : j + 1],
+                            op0=ALU.mult,
+                            op1=ALU.add,
+                        )
+                    else:
+                        nc.scalar.activation(
+                            out=y[:, j, :],
+                            in_=acc[:, h, :],
+                            func=ACT.Identity,
+                            bias=offset[b][:, w, j : j + 1],
+                            scale=inverse[b][:, w, j : j + 1],
+                        )
+                done = BANK_TILES * (bank + 1)
+                if done % STORE_TILES == 0:
+                    nc.sync.dma_start(
+                        out=out_view[:, done - STORE_TILES : done, :], in_=y[:, done - STORE_TILES : done, :]
+                    )
+
+        prepare(0)
+        prepare(1)
+        for b in range(IMAGES):
+            convolve(b, 0)
+            if b + 2 < IMAGES:
+                prepare(b + 2)
+            convolve(b, 1)

@@ -42,17 +42,26 @@ def tile_wb_pa_kernel(tc, x, Wc_words, Wc_scales, bc, W1_words, W1_scales, b1, o
     outs = (out_0, out_1)
 
     with ExitStack() as ctx:
+        ctx.enter_context(tc.manual_schedule())
         const = ctx.enter_context(tc.tile_pool(name="const", bufs=1))
         image = ctx.enter_context(tc.tile_pool(name="image", bufs=1))
         result = ctx.enter_context(tc.tile_pool(name="result", bufs=1))
-        acc_psum = ctx.enter_context(tc.psum_pool(name="acc_psum", bufs=4))
-        sum_psum = ctx.enter_context(tc.psum_pool(name="sum_psum", bufs=2))
+        acc_psum = ctx.enter_context(tc.psum_pool(name="acc_psum", bufs=5))
         small_psum = ctx.enter_context(tc.psum_pool(name="small_psum", bufs=1))
 
         w_planes = const.tile([P, CHANNELS], U8, align_bytes=64)
         nc.vector.memset(w_planes[:].bitcast(I32), 0)
         bias_rows = const.tile([P, P], BF16)
         nc.vector.memset(bias_rows[:], 0.0)
+        ident_bf = const.tile([P, P], BF16)
+        nc.vector.memset(ident_bf[:], 0.0)
+        make_identity(nc, ident_bf[:], nomemset=True)
+
+        for w in range(2):
+            nc.scalar.dma_start(
+                out=bias_rows[O_TILES * w : O_TILES * (w + 1), :],
+                in_=bias_in[w].rearrange("(j m) -> j m", m=P),
+            )
 
         x_sb = []
         for b in range(IMAGES):
@@ -75,16 +84,8 @@ def tile_wb_pa_kernel(tc, x, Wc_words, Wc_scales, bc, W1_words, W1_scales, b1, o
             nc.sync.dma_start(out=words[:], in_=words_in[w].rearrange("g p n t -> p g (n t)").bitcast(I32))
             w_words.append(words)
 
-        ident_bf = const.tile([P, P], BF16)
-        make_identity(nc, ident_bf[:])
         ident = const.tile([P, P], F32)
-        make_identity(nc, ident[:])
-        for w in range(2):
-            nc.gpsimd.dma_start(
-                out=bias_rows[O_TILES * w : O_TILES * (w + 1), :],
-                in_=bias_in[w].rearrange("(j m) -> j m", m=P),
-            )
-
+        nc.vector.tensor_copy(out=ident[:], in_=ident_bf[:])
         same_r = const.tile([P, IN_QUADRANT], F32)
         nc.vector.tensor_reduce(
             out=same_r[:], in_=ident[:].rearrange("p (q r) -> p r q", q=QUADRANTS), axis=AX.X, op=ALU.add
@@ -108,28 +109,29 @@ def tile_wb_pa_kernel(tc, x, Wc_words, Wc_scales, bc, W1_words, W1_scales, b1, o
         bias = const.tile([P, 2, O_TILES], F32)
         nc.vector.tensor_copy(out=bias[:].rearrange("p w j -> p (w j)"), in_=bias_t[:, 0 : 2 * O_TILES])
 
-        x_codes = []
-        x_planes = []
-        inverse = []
-        offset = []
+        stat = const.tile([P, 2, IMAGES, ROWS], F32)
+        sums = small_psum.tile([P, IMAGES, ROWS, SUM_CHUNK], F32)
+        moved = small_psum.tile([P, IMAGES, QUADRANTS * 2 * PASSES], F32)
+        masked = const.tile([P, IMAGES, QUADRANTS * 2 * PASSES, PACK], F32)
+        x_codes = const.tile([P, IMAGES, PASSES, PIXELS], U32, align_bytes=64)
+        x_planes = const.tile([P, IMAGES, PASSES, PIXELS], U8, align_bytes=64)
+        divisor = const.tile([P, IMAGES, 2, O_TILES], F32)
+        inverse = const.tile([P, IMAGES, 2, O_TILES], F32)
+        offset = const.tile([P, IMAGES, 2, O_TILES], F32)
 
-        def prepare(b):
-            x_b = x_sb[b]
-            stat = image.tile([P, 2, ROWS], F32, name="stat%d" % b)
-
-            sums = sum_psum.tile([P, ROWS, SUM_CHUNK], F32, name="sums")
+        def add_pixels(b):
             chunks = PIXELS // SUM_CHUNK
             for c in range(chunks):
                 nc.tensor.matmul(
-                    out=sums[:],
+                    out=sums[:, b],
                     lhsT=ident_bf[:],
-                    rhs=x_b[:, :, SUM_CHUNK * c : SUM_CHUNK * (c + 1)],
+                    rhs=x_sb[b][:, :, SUM_CHUNK * c : SUM_CHUNK * (c + 1)],
                     start=(c == 0),
                     stop=(c == chunks - 1),
                 )
-            nc.vector.tensor_reduce(out=stat[:, 0, :], in_=sums[:], axis=AX.X, op=ALU.add)
 
-            widest = x_b
+        def maxima(b):
+            widest = x_sb[b]
             for halving in range(1, MAX_HALVINGS + 1):
                 width = PIXELS >> halving
                 narrower = image.tile([P, ROWS, width], BF16, name="max%d_%d" % (b, width))
@@ -137,56 +139,48 @@ def tile_wb_pa_kernel(tc, x, Wc_words, Wc_scales, bc, W1_words, W1_scales, b1, o
                     out=narrower[:], in0=widest[:, :, 0:width], in1=widest[:, :, width : 2 * width], op=ALU.max
                 )
                 widest = narrower
-            nc.vector.tensor_reduce(out=stat[:, 1, :], in_=widest[:], axis=AX.X, op=ALU.max)
+            nc.vector.tensor_reduce(out=stat[:, 1, b, :], in_=widest[:], axis=AX.X, op=ALU.max)
 
-            masked = image.tile([P, QUADRANTS * 2 * PASSES, PACK], F32, name="masked%d" % b)
-            shape = [P, QUADRANTS, 2, ROWS]
-            nc.vector.tensor_tensor(
-                out=masked[:].rearrange("p (q s g) t -> p q s (g t)", q=QUADRANTS, s=2),
-                in0=stat[:].unsqueeze(1).to_broadcast(shape),
-                in1=pick[:].unsqueeze(3).to_broadcast(shape),
-                op=ALU.mult,
-            )
-            moved = small_psum.tile([P, QUADRANTS * 2 * PASSES], F32, name="moved")
-            for t in range(PACK):
-                nc.tensor.matmul(
-                    out=moved[:],
-                    lhsT=spread[:, t].rearrange("p r u -> p (r u)"),
-                    rhs=masked[:, :, t],
-                    start=(t == 0),
-                    stop=(t == PACK - 1),
-                )
-
+        def quantise(b):
             grouped = image.tile([P, PASSES, PIXELS, PACK], BF16, name="grouped%d" % b, align_bytes=64)
             for g in range(PASSES):
                 nc.vector.tensor_copy(
                     out=grouped[:, g].rearrange("p (c i) t -> p c t i", i=4),
-                    in_=x_b[:, PACK * g : PACK * (g + 1), :].rearrange("p t (c i) -> p c t i", i=4),
+                    in_=x_sb[b][:, PACK * g : PACK * (g + 1), :].rearrange("p t (c i) -> p c t i", i=4),
                 )
-            codes = image.tile([P, PASSES * PIXELS], U32, name="codes%d" % b, align_bytes=64)
-            plane = image.tile([P, PASSES * PIXELS], U8, name="plane%d" % b, align_bytes=64)
             nc.vector.quantize_mx(
-                out=codes[:].bitcast(FP8X4),
-                scales=plane[:],
+                out=x_codes[:, b].rearrange("p g n -> p (g n)").bitcast(FP8X4),
+                scales=x_planes[:, b].rearrange("p g n -> p (g n)"),
                 in_=grouped[:].rearrange("p g n t -> p (g n t)"),
             )
-            x_codes.append(codes)
-            x_planes.append(plane)
 
-            divisor = image.tile([P, 2, O_TILES], F32, name="divisor%d" % b)
+        def mask(b):
+            shape = [P, QUADRANTS, 2, ROWS]
+            nc.vector.tensor_tensor(
+                out=masked[:, b].rearrange("p (q s g) t -> p q s (g t)", q=QUADRANTS, s=2),
+                in0=stat[:, :, b, :].unsqueeze(1).to_broadcast(shape),
+                in1=pick[:].unsqueeze(3).to_broadcast(shape),
+                op=ALU.mult,
+            )
+
+        def divisors(b):
+            for t in range(PACK):
+                nc.tensor.matmul(
+                    out=moved[:, b],
+                    lhsT=spread[:, t].rearrange("p r u -> p (r u)"),
+                    rhs=masked[:, b, :, t],
+                    start=(t == 0),
+                    stop=(t == PACK - 1),
+                )
             nc.vector.tensor_scalar(
-                out=divisor[:].rearrange("p s (g q) -> p q s g", q=QUADRANTS),
-                in0=moved[:].rearrange("p (q s g) -> p q s g", q=QUADRANTS, s=2),
+                out=divisor[:, b].rearrange("p s (g q) -> p q s g", q=QUADRANTS),
+                in0=moved[:, b].rearrange("p (q s g) -> p q s g", q=QUADRANTS, s=2),
                 scalar1=EPS,
                 scalar2=None,
                 op0=ALU.add,
             )
-            inverse_b = image.tile([P, 2, O_TILES], F32, name="inverse%d" % b)
-            nc.vector.reciprocal(out=inverse_b[:], in_=divisor[:])
-            offset_b = image.tile([P, 2, O_TILES], F32, name="offset%d" % b)
-            nc.vector.tensor_tensor(out=offset_b[:], in0=bias[:], in1=inverse_b[:], op=ALU.mult)
-            inverse.append(inverse_b)
-            offset.append(offset_b)
+            nc.vector.reciprocal(out=inverse[:, b], in_=divisor[:, b])
+            nc.vector.tensor_tensor(out=offset[:, b], in0=bias[:], in1=inverse[:, b], op=ALU.mult)
 
         def convolve(b, w):
             y = result.tile([P, O_TILES, PIXELS], F32, name="y%d_%d" % (b, w))
@@ -200,8 +194,8 @@ def tile_wb_pa_kernel(tc, x, Wc_words, Wc_scales, bc, W1_words, W1_scales, b1, o
                             out=acc[:, h, :],
                             lhsT=w_words[w][:, g, P * j : P * (j + 1)].bitcast(FP8X4),
                             lhsT_scale=w_planes[PACK * (PASSES * w + g) : P, P * j : P * (j + 1)],
-                            rhs=x_codes[b][:, PIXELS * g : PIXELS * (g + 1)].bitcast(FP8X4),
-                            rhs_scale=x_planes[b][:, PIXELS * g : PIXELS * (g + 1)],
+                            rhs=x_codes[:, b, g, :].bitcast(FP8X4),
+                            rhs_scale=x_planes[:, b, g, :],
                             start=(g == 0),
                             stop=(g == PASSES - 1),
                         )
@@ -211,8 +205,8 @@ def tile_wb_pa_kernel(tc, x, Wc_words, Wc_scales, bc, W1_words, W1_scales, b1, o
                         nc.vector.tensor_scalar(
                             out=y[:, j, :],
                             in0=acc[:, h, :],
-                            scalar1=inverse[b][:, w, j : j + 1],
-                            scalar2=offset[b][:, w, j : j + 1],
+                            scalar1=inverse[:, b, w, j : j + 1],
+                            scalar2=offset[:, b, w, j : j + 1],
                             op0=ALU.mult,
                             op1=ALU.add,
                         )
@@ -221,8 +215,8 @@ def tile_wb_pa_kernel(tc, x, Wc_words, Wc_scales, bc, W1_words, W1_scales, b1, o
                             out=y[:, j, :],
                             in_=acc[:, h, :],
                             func=ACT.Identity,
-                            bias=offset[b][:, w, j : j + 1],
-                            scale=inverse[b][:, w, j : j + 1],
+                            bias=offset[:, b, w, j : j + 1],
+                            scale=inverse[:, b, w, j : j + 1],
                         )
                 done = BANK_TILES * (bank + 1)
                 if done % STORE_TILES == 0:
@@ -230,10 +224,21 @@ def tile_wb_pa_kernel(tc, x, Wc_words, Wc_scales, bc, W1_words, W1_scales, b1, o
                         out=out_view[:, done - STORE_TILES : done, :], in_=y[:, done - STORE_TILES : done, :]
                     )
 
-        prepare(0)
-        prepare(1)
         for b in range(IMAGES):
-            convolve(b, 0)
+            add_pixels(b)
+        maxima(0)
+        quantise(0)
+        maxima(1)
+        nc.vector.tensor_reduce(out=stat[:, 0], in_=sums[:], axis=AX.X, op=ALU.add)
+        mask(0)
+        divisors(0)
+        for b in range(IMAGES):
+            if b + 1 < IMAGES:
+                mask(b + 1)
+                quantise(b + 1)
             if b + 2 < IMAGES:
-                prepare(b + 2)
+                maxima(b + 2)
+            convolve(b, 0)
+            if b + 1 < IMAGES:
+                divisors(b + 1)
             convolve(b, 1)

@@ -46,7 +46,7 @@ def tile_wb_pa_kernel(tc, x, Wc_words, Wc_scales, bc, W1_words, W1_scales, b1, o
         const = ctx.enter_context(tc.tile_pool(name="const", bufs=1))
         image = ctx.enter_context(tc.tile_pool(name="image", bufs=1))
         result = ctx.enter_context(tc.tile_pool(name="result", bufs=1))
-        acc_psum = ctx.enter_context(tc.psum_pool(name="acc_psum", bufs=5))
+        acc_psum = ctx.enter_context(tc.psum_pool(name="acc_psum", bufs=6))
         small_psum = ctx.enter_context(tc.psum_pool(name="small_psum", bufs=1))
 
         w_planes = const.tile([P, CHANNELS], U8, align_bytes=64)
@@ -104,13 +104,9 @@ def tile_wb_pa_kernel(tc, x, Wc_words, Wc_scales, bc, W1_words, W1_scales, b1, o
         )
         nc.vector.tensor_copy(out=pick[:, :, 1:2], in_=same_q[:].unsqueeze(2))
 
-        bias_t = small_psum.tile([P, P], BF16)
-        nc.tensor.transpose(bias_t[:], bias_rows[:], ident_bf[:])
         bias = const.tile([P, 2, O_TILES], F32)
-        nc.vector.tensor_copy(out=bias[:].rearrange("p w j -> p (w j)"), in_=bias_t[:, 0 : 2 * O_TILES])
 
         stat = const.tile([P, 2, IMAGES, ROWS], F32)
-        sums = small_psum.tile([P, IMAGES, ROWS, SUM_CHUNK], F32)
         moved = small_psum.tile([P, IMAGES, QUADRANTS * 2 * PASSES], F32)
         masked = const.tile([P, IMAGES, QUADRANTS * 2 * PASSES, PACK], F32)
         x_codes = const.tile([P, IMAGES, PASSES, PIXELS], U32, align_bytes=64)
@@ -119,18 +115,23 @@ def tile_wb_pa_kernel(tc, x, Wc_words, Wc_scales, bc, W1_words, W1_scales, b1, o
         inverse = const.tile([P, IMAGES, 2, O_TILES], F32)
         offset = const.tile([P, IMAGES, 2, O_TILES], F32)
 
+        sums = []
+        grouped = []
+
         def add_pixels(b):
+            sums_b = acc_psum.tile([P, ROWS, SUM_CHUNK], F32, name="sums", tag="acc")
             chunks = PIXELS // SUM_CHUNK
             for c in range(chunks):
                 nc.tensor.matmul(
-                    out=sums[:, b],
+                    out=sums_b[:],
                     lhsT=ident_bf[:],
                     rhs=x_sb[b][:, :, SUM_CHUNK * c : SUM_CHUNK * (c + 1)],
                     start=(c == 0),
                     stop=(c == chunks - 1),
                 )
+            sums.append(sums_b)
 
-        def maxima(b):
+        def statistics(b):
             widest = x_sb[b]
             for halving in range(1, MAX_HALVINGS + 1):
                 width = PIXELS >> halving
@@ -140,18 +141,22 @@ def tile_wb_pa_kernel(tc, x, Wc_words, Wc_scales, bc, W1_words, W1_scales, b1, o
                 )
                 widest = narrower
             nc.vector.tensor_reduce(out=stat[:, 1, b, :], in_=widest[:], axis=AX.X, op=ALU.max)
+            nc.vector.tensor_reduce(out=stat[:, 0, b, :], in_=sums[b][:], axis=AX.X, op=ALU.add)
 
-        def quantise(b):
-            grouped = image.tile([P, PASSES, PIXELS, PACK], BF16, name="grouped%d" % b, align_bytes=64)
+        def regroup(b, copy):
+            grouped_b = image.tile([P, PASSES, PIXELS, PACK], BF16, name="grouped%d" % b, align_bytes=64)
             for g in range(PASSES):
-                nc.vector.tensor_copy(
-                    out=grouped[:, g].rearrange("p (c i) t -> p c t i", i=4),
+                copy(
+                    out=grouped_b[:, g].rearrange("p (c i) t -> p c t i", i=4),
                     in_=x_sb[b][:, PACK * g : PACK * (g + 1), :].rearrange("p t (c i) -> p c t i", i=4),
                 )
+            grouped.append(grouped_b)
+
+        def quantise(b):
             nc.vector.quantize_mx(
                 out=x_codes[:, b].rearrange("p g n -> p (g n)").bitcast(FP8X4),
                 scales=x_planes[:, b].rearrange("p g n -> p (g n)"),
-                in_=grouped[:].rearrange("p g n t -> p (g n t)"),
+                in_=grouped[b][:].rearrange("p g n t -> p (g n t)"),
             )
 
         def mask(b):
@@ -163,7 +168,7 @@ def tile_wb_pa_kernel(tc, x, Wc_words, Wc_scales, bc, W1_words, W1_scales, b1, o
                 op=ALU.mult,
             )
 
-        def divisors(b):
+        def move(b):
             for t in range(PACK):
                 nc.tensor.matmul(
                     out=moved[:, b],
@@ -172,6 +177,8 @@ def tile_wb_pa_kernel(tc, x, Wc_words, Wc_scales, bc, W1_words, W1_scales, b1, o
                     start=(t == 0),
                     stop=(t == PACK - 1),
                 )
+
+        def invert(b):
             nc.vector.tensor_scalar(
                 out=divisor[:, b].rearrange("p s (g q) -> p q s g", q=QUADRANTS),
                 in0=moved[:, b].rearrange("p (q s g) -> p q s g", q=QUADRANTS, s=2),
@@ -186,7 +193,7 @@ def tile_wb_pa_kernel(tc, x, Wc_words, Wc_scales, bc, W1_words, W1_scales, b1, o
             y = result.tile([P, O_TILES, PIXELS], F32, name="y%d_%d" % (b, w))
             out_view = outs[w][b].rearrange("(j m) h w -> m j (h w)", m=P)
             for bank in range(O_TILES // BANK_TILES):
-                acc = acc_psum.tile([P, BANK_TILES, PIXELS], F32, name="acc")
+                acc = acc_psum.tile([P, BANK_TILES, PIXELS], F32, name="acc", tag="acc")
                 for h in range(BANK_TILES):
                     j = BANK_TILES * bank + h
                     for g in range(PASSES):
@@ -224,21 +231,32 @@ def tile_wb_pa_kernel(tc, x, Wc_words, Wc_scales, bc, W1_words, W1_scales, b1, o
                         out=out_view[:, done - STORE_TILES : done, :], in_=y[:, done - STORE_TILES : done, :]
                     )
 
-        for b in range(IMAGES):
-            add_pixels(b)
-        maxima(0)
+        add_pixels(0)
+        add_pixels(1)
+        bias_t = small_psum.tile([P, P], BF16)
+        nc.tensor.transpose(bias_t[:], bias_rows[:], ident_bf[:])
+        regroup(0, nc.vector.tensor_copy)
+        for b in range(1, IMAGES):
+            regroup(b, nc.scalar.copy)
         quantise(0)
-        maxima(1)
-        nc.vector.tensor_reduce(out=stat[:, 0], in_=sums[:], axis=AX.X, op=ALU.add)
+        statistics(0)
         mask(0)
-        divisors(0)
+        move(0)
+        add_pixels(2)
+        add_pixels(3)
+        statistics(1)
+        nc.vector.tensor_copy(out=bias[:].rearrange("p w j -> p (w j)"), in_=bias_t[:, 0 : 2 * O_TILES])
+        invert(0)
+        quantise(1)
+        mask(1)
+        statistics(2)
+        statistics(3)
         for b in range(IMAGES):
-            if b + 1 < IMAGES:
-                mask(b + 1)
-                quantise(b + 1)
-            if b + 2 < IMAGES:
-                maxima(b + 2)
             convolve(b, 0)
             if b + 1 < IMAGES:
-                divisors(b + 1)
+                move(b + 1)
+                invert(b + 1)
+            if b + 2 < IMAGES:
+                quantise(b + 2)
+                mask(b + 2)
             convolve(b, 1)

@@ -20,16 +20,16 @@ EPS = 1e-05
 
 P = 128
 PACK = 4
-PASSES = CHANNELS // (P * PACK)
+K_PASS = P * PACK
+PASSES = CHANNELS // K_PASS
+HALVES = CHANNELS // K_PASS
 ROWS = PASSES * PACK
-O_TILES = CHANNELS // P
+O_TILES = HALVES * PACK
 QUADRANTS = 4
 IN_QUADRANT = P // QUADRANTS
 SUM_CHUNK = 16
 BANK_TILES = 2
-STORE_TILES = 4
 MAX_HALVINGS = 3
-VECTOR_EVERY = 4
 
 FLOPS = 2 * 2 * CHANNELS * CHANNELS * IMAGES * PIXELS
 
@@ -46,22 +46,20 @@ def tile_wb_pa_kernel(tc, x, Wc_words, Wc_scales, bc, W1_words, W1_scales, b1, o
         const = ctx.enter_context(tc.tile_pool(name="const", bufs=1))
         image = ctx.enter_context(tc.tile_pool(name="image", bufs=1))
         result = ctx.enter_context(tc.tile_pool(name="result", bufs=1))
-        acc_psum = ctx.enter_context(tc.psum_pool(name="acc_psum", bufs=6))
-        small_psum = ctx.enter_context(tc.psum_pool(name="small_psum", bufs=1))
+        acc_psum = ctx.enter_context(tc.psum_pool(name="acc_psum", bufs=7))
+        sum_psum = ctx.enter_context(tc.psum_pool(name="sum_psum", bufs=1))
 
-        w_planes = const.tile([P, CHANNELS], U8, align_bytes=64)
-        nc.vector.memset(w_planes[:].bitcast(I32), 0)
-        bias_rows = const.tile([P, P], BF16)
-        nc.vector.memset(bias_rows[:], 0.0)
-        ident_bf = const.tile([P, P], BF16)
-        nc.vector.memset(ident_bf[:], 0.0)
-        make_identity(nc, ident_bf[:], nomemset=True)
+        planes_in = const.tile([P, CHANNELS], U8)
+        nc.vector.memset(planes_in[:].bitcast(I32), 0)
+        ident = const.tile([P, P], BF16)
+        nc.vector.memset(ident[:], 0.0)
+        make_identity(nc, ident[:], nomemset=True)
 
+        bias_bf = []
         for w in range(2):
-            nc.scalar.dma_start(
-                out=bias_rows[O_TILES * w : O_TILES * (w + 1), :],
-                in_=bias_in[w].rearrange("(j m) -> j m", m=P),
-            )
+            bias_w = const.tile([P, HALVES, PACK], BF16, name="bias_bf%d" % w)
+            nc.scalar.dma_start(out=bias_w[:], in_=bias_in[w].rearrange("(h p t) -> p h t", h=HALVES, p=P, t=PACK))
+            bias_bf.append(bias_w)
 
         x_sb = []
         for b in range(IMAGES):
@@ -72,76 +70,76 @@ def tile_wb_pa_kernel(tc, x, Wc_words, Wc_scales, bc, W1_words, W1_scales, b1, o
             )
             x_sb.append(x_b)
 
-        w_words = []
         for w in range(2):
             for quadrant in range(QUADRANTS):
                 first = IN_QUADRANT * quadrant + PACK * PASSES * w
                 nc.sync.dma_start(
-                    out=w_planes[first : first + PACK * PASSES, :].bitcast(I32),
+                    out=planes_in[first : first + PACK * PASSES, :].bitcast(I32),
                     in_=scales_in[w][:, PACK * quadrant : PACK * (quadrant + 1), :].bitcast(I32),
                 )
-            words = const.tile([P, PASSES, CHANNELS], I32, name="words%d" % w, align_bytes=64)
-            nc.sync.dma_start(out=words[:], in_=words_in[w].rearrange("g p n t -> p g (n t)").bitcast(I32))
-            w_words.append(words)
+        words_sb = []
+        for w in range(2):
+            words_w = const.tile([P, PASSES, CHANNELS], I32, name="words_in%d" % w)
+            nc.sync.dma_start(out=words_w[:], in_=words_in[w].rearrange("g p n t -> p g (n t)").bitcast(I32))
+            words_sb.append(words_w)
 
-        ident = const.tile([P, P], F32)
-        nc.vector.tensor_copy(out=ident[:], in_=ident_bf[:])
-        same_r = const.tile([P, IN_QUADRANT], F32)
-        nc.vector.tensor_reduce(
-            out=same_r[:], in_=ident[:].rearrange("p (q r) -> p r q", q=QUADRANTS), axis=AX.X, op=ALU.add
-        )
-        spread = const.tile([P, PACK, IN_QUADRANT, PACK], F32)
-        nc.vector.memset(spread[:], 0.0)
-        for t in range(PACK):
-            nc.vector.tensor_copy(out=spread[:, t, :, t : t + 1], in_=same_r[:].unsqueeze(2))
-        same_q = const.tile([P, QUADRANTS], F32)
-        nc.vector.tensor_reduce(
-            out=same_q[:], in_=ident[:].rearrange("p (q r) -> p q r", q=QUADRANTS), axis=AX.X, op=ALU.add
-        )
-        pick = const.tile([P, QUADRANTS, 2], F32)
-        nc.vector.tensor_scalar(
-            out=pick[:, :, 0:1], in0=same_q[:].unsqueeze(2), scalar1=1.0 / PIXELS, scalar2=None, op0=ALU.mult
-        )
-        nc.vector.tensor_copy(out=pick[:, :, 1:2], in_=same_q[:].unsqueeze(2))
-
+        averager = const.tile([P, P], BF16)
+        nc.vector.tensor_scalar(out=averager[:], in0=ident[:], scalar1=1.0 / PIXELS, scalar2=None, op0=ALU.mult)
         bias = const.tile([P, 2, O_TILES], F32)
 
+        w_planes = const.tile([P, CHANNELS], U8, align_bytes=64)
+        w_words = [
+            const.tile([P, HALVES, PASSES, PACK, P], I32, name="w_words%d" % w, align_bytes=64) for w in range(2)
+        ]
+
         stat = const.tile([P, 2, IMAGES, ROWS], F32)
-        moved = small_psum.tile([P, IMAGES, QUADRANTS * 2 * PASSES], F32)
-        masked = const.tile([P, IMAGES, QUADRANTS * 2 * PASSES, PACK], F32)
+        sums = sum_psum.tile([P, IMAGES, ROWS, SUM_CHUNK], F32)
         x_codes = const.tile([P, IMAGES, PASSES, PIXELS], U32, align_bytes=64)
         x_planes = const.tile([P, IMAGES, PASSES, PIXELS], U8, align_bytes=64)
         divisor = const.tile([P, IMAGES, 2, O_TILES], F32)
         inverse = const.tile([P, IMAGES, 2, O_TILES], F32)
         offset = const.tile([P, IMAGES, 2, O_TILES], F32)
 
-        sums = []
-        grouped = []
+        grouped = {}
+        narrowed = {}
+
+        def permute_planes():
+            nc.vector.tensor_copy(
+                out=w_planes[:].rearrange("p (h t m) -> p h m t", h=HALVES, t=PACK),
+                in_=planes_in[:].rearrange("p (h m t) -> p h m t", h=HALVES, t=PACK),
+            )
+
+        def permute_words(w, h):
+            nc.vector.tensor_copy(
+                out=w_words[w][:, h].rearrange("p g t m -> p g m t"),
+                in_=words_sb[w][:, :, K_PASS * h : K_PASS * (h + 1)].rearrange("p g (m t) -> p g m t", t=PACK),
+            )
 
         def add_pixels(b):
-            sums_b = acc_psum.tile([P, ROWS, SUM_CHUNK], F32, name="sums", tag="acc")
             chunks = PIXELS // SUM_CHUNK
             for c in range(chunks):
                 nc.tensor.matmul(
-                    out=sums_b[:],
-                    lhsT=ident_bf[:],
+                    out=sums[:, b],
+                    lhsT=averager[:],
                     rhs=x_sb[b][:, :, SUM_CHUNK * c : SUM_CHUNK * (c + 1)],
                     start=(c == 0),
                     stop=(c == chunks - 1),
                 )
-            sums.append(sums_b)
 
-        def statistics(b):
-            widest = x_sb[b]
-            for halving in range(1, MAX_HALVINGS + 1):
-                width = PIXELS >> halving
-                narrower = image.tile([P, ROWS, width], BF16, name="max%d_%d" % (b, width))
-                nc.vector.tensor_tensor(
-                    out=narrower[:], in0=widest[:, :, 0:width], in1=widest[:, :, width : 2 * width], op=ALU.max
-                )
-                widest = narrower
-            nc.vector.tensor_reduce(out=stat[:, 1, b, :], in_=widest[:], axis=AX.X, op=ALU.max)
-            nc.vector.tensor_reduce(out=stat[:, 0, b, :], in_=sums[b][:], axis=AX.X, op=ALU.add)
+        def halve(b, halving):
+            widest = x_sb[b] if halving == 1 else narrowed[b]
+            width = PIXELS >> halving
+            narrower = image.tile([P, ROWS, width], BF16, name="max%d_%d" % (b, width))
+            nc.vector.tensor_tensor(
+                out=narrower[:], in0=widest[:, :, 0:width], in1=widest[:, :, width : 2 * width], op=ALU.max
+            )
+            narrowed[b] = narrower
+
+        def finish_statistics(b):
+            for halving in range(2, MAX_HALVINGS + 1):
+                halve(b, halving)
+            nc.vector.tensor_reduce(out=stat[:, 1, b, :], in_=narrowed[b][:], axis=AX.X, op=ALU.max)
+            nc.vector.tensor_reduce(out=stat[:, 0, b, :], in_=sums[:, b], axis=AX.X, op=ALU.add)
 
         def regroup(b, copy):
             grouped_b = image.tile([P, PASSES, PIXELS, PACK], BF16, name="grouped%d" % b, align_bytes=64)
@@ -150,7 +148,7 @@ def tile_wb_pa_kernel(tc, x, Wc_words, Wc_scales, bc, W1_words, W1_scales, b1, o
                     out=grouped_b[:, g].rearrange("p (c i) t -> p c t i", i=4),
                     in_=x_sb[b][:, PACK * g : PACK * (g + 1), :].rearrange("p t (c i) -> p c t i", i=4),
                 )
-            grouped.append(grouped_b)
+            grouped[b] = grouped_b
 
         def quantise(b):
             nc.vector.quantize_mx(
@@ -159,59 +157,36 @@ def tile_wb_pa_kernel(tc, x, Wc_words, Wc_scales, bc, W1_words, W1_scales, b1, o
                 in_=grouped[b][:].rearrange("p g n t -> p (g n t)"),
             )
 
-        def mask(b):
-            shape = [P, QUADRANTS, 2, ROWS]
-            nc.vector.tensor_tensor(
-                out=masked[:, b].rearrange("p (q s g) t -> p q s (g t)", q=QUADRANTS, s=2),
-                in0=stat[:, :, b, :].unsqueeze(1).to_broadcast(shape),
-                in1=pick[:].unsqueeze(3).to_broadcast(shape),
-                op=ALU.mult,
-            )
-
-        def move(b):
-            for t in range(PACK):
-                nc.tensor.matmul(
-                    out=moved[:, b],
-                    lhsT=spread[:, t].rearrange("p r u -> p (r u)"),
-                    rhs=masked[:, b, :, t],
-                    start=(t == 0),
-                    stop=(t == PACK - 1),
-                )
-
         def invert(b):
             nc.vector.tensor_scalar(
-                out=divisor[:, b].rearrange("p s (g q) -> p q s g", q=QUADRANTS),
-                in0=moved[:, b].rearrange("p (q s g) -> p q s g", q=QUADRANTS, s=2),
-                scalar1=EPS,
-                scalar2=None,
-                op0=ALU.add,
+                out=divisor[:, b], in0=stat[:, :, b, :], scalar1=EPS, scalar2=None, op0=ALU.add
             )
             nc.vector.reciprocal(out=inverse[:, b], in_=divisor[:, b])
             nc.vector.tensor_tensor(out=offset[:, b], in0=bias[:], in1=inverse[:, b], op=ALU.mult)
 
-        def convolve(b, w):
+        def convolve(b, w, vector_banks):
             y = result.tile([P, O_TILES, PIXELS], F32, name="y%d_%d" % (b, w))
-            out_view = outs[w][b].rearrange("(j m) h w -> m j (h w)", m=P)
+            out_view = outs[w][b].rearrange("(h p t) r c -> p h (t r c)", h=HALVES, p=P, t=PACK)
             for bank in range(O_TILES // BANK_TILES):
                 acc = acc_psum.tile([P, BANK_TILES, PIXELS], F32, name="acc", tag="acc")
-                for h in range(BANK_TILES):
-                    j = BANK_TILES * bank + h
+                for i in range(BANK_TILES):
+                    h, t = divmod(BANK_TILES * bank + i, PACK)
                     for g in range(PASSES):
                         nc.tensor.matmul_mx(
-                            out=acc[:, h, :],
-                            lhsT=w_words[w][:, g, P * j : P * (j + 1)].bitcast(FP8X4),
-                            lhsT_scale=w_planes[PACK * (PASSES * w + g) : P, P * j : P * (j + 1)],
+                            out=acc[:, i, :],
+                            lhsT=w_words[w][:, h, g, t, :].bitcast(FP8X4),
+                            lhsT_scale=w_planes[PACK * (PASSES * w + g) : P, K_PASS * h + P * t : K_PASS * h + P * (t + 1)],
                             rhs=x_codes[:, b, g, :].bitcast(FP8X4),
                             rhs_scale=x_planes[:, b, g, :],
                             start=(g == 0),
                             stop=(g == PASSES - 1),
                         )
-                for h in range(BANK_TILES):
-                    j = BANK_TILES * bank + h
-                    if bank % VECTOR_EVERY == VECTOR_EVERY - 1:
+                for i in range(BANK_TILES):
+                    j = BANK_TILES * bank + i
+                    if bank in vector_banks:
                         nc.vector.tensor_scalar(
                             out=y[:, j, :],
-                            in0=acc[:, h, :],
+                            in0=acc[:, i, :],
                             scalar1=inverse[:, b, w, j : j + 1],
                             scalar2=offset[:, b, w, j : j + 1],
                             op0=ALU.mult,
@@ -220,43 +195,52 @@ def tile_wb_pa_kernel(tc, x, Wc_words, Wc_scales, bc, W1_words, W1_scales, b1, o
                     else:
                         nc.scalar.activation(
                             out=y[:, j, :],
-                            in_=acc[:, h, :],
+                            in_=acc[:, i, :],
                             func=ACT.Identity,
                             bias=offset[:, b, w, j : j + 1],
                             scale=inverse[:, b, w, j : j + 1],
                         )
                 done = BANK_TILES * (bank + 1)
-                if done % STORE_TILES == 0:
+                if done % PACK == 0:
+                    h = done // PACK - 1
                     nc.sync.dma_start(
-                        out=out_view[:, done - STORE_TILES : done, :], in_=y[:, done - STORE_TILES : done, :]
+                        out=out_view[:, h, :], in_=y[:, PACK * h : PACK * (h + 1), :].rearrange("p t n -> p (t n)")
                     )
 
-        add_pixels(0)
-        add_pixels(1)
-        bias_t = small_psum.tile([P, P], BF16)
-        nc.tensor.transpose(bias_t[:], bias_rows[:], ident_bf[:])
-        regroup(0, nc.vector.tensor_copy)
-        for b in range(1, IMAGES):
-            regroup(b, nc.scalar.copy)
-        quantise(0)
-        statistics(0)
-        mask(0)
-        move(0)
-        add_pixels(2)
-        add_pixels(3)
-        statistics(1)
-        nc.vector.tensor_copy(out=bias[:].rearrange("p w j -> p (w j)"), in_=bias_t[:, 0 : 2 * O_TILES])
-        invert(0)
-        quantise(1)
-        mask(1)
-        statistics(2)
-        statistics(3)
         for b in range(IMAGES):
-            convolve(b, 0)
-            if b + 1 < IMAGES:
-                move(b + 1)
-                invert(b + 1)
-            if b + 2 < IMAGES:
-                quantise(b + 2)
-                mask(b + 2)
-            convolve(b, 1)
+            add_pixels(b)
+        regroup(0, nc.vector.tensor_copy)
+        regroup(1, nc.scalar.copy)
+        regroup(2, nc.scalar.copy)
+        halve(0, 1)
+        quantise(0)
+        for w in range(2):
+            nc.vector.tensor_copy(out=bias[:, w, :], in_=bias_bf[w][:].rearrange("p h t -> p (h t)"))
+        finish_statistics(0)
+        invert(0)
+        permute_planes()
+        quantise(1)
+        permute_words(0, 0)
+        permute_words(0, 1)
+        halve(1, 1)
+        permute_words(1, 0)
+        permute_words(1, 1)
+        convolve(0, 0, ())
+        finish_statistics(1)
+        invert(1)
+        regroup(3, nc.vector.tensor_copy)
+        convolve(0, 1, ())
+        quantise(2)
+        halve(2, 1)
+        convolve(1, 0, (3,))
+        finish_statistics(2)
+        invert(2)
+        quantise(3)
+        convolve(1, 1, (3,))
+        halve(3, 1)
+        convolve(2, 0, (3,))
+        finish_statistics(3)
+        invert(3)
+        convolve(2, 1, (3,))
+        convolve(3, 0, (3,))
+        convolve(3, 1, (3,))

@@ -49,20 +49,21 @@ def tile_wb_pa_kernel(tc, x, Wc_words, Wc_scales, bc, W1_words, W1_scales, b1, o
         acc_psum = ctx.enter_context(tc.psum_pool(name="acc_psum", bufs=7))
         sum_psum = ctx.enter_context(tc.psum_pool(name="sum_psum", bufs=1))
 
-        planes_in = const.tile([P, CHANNELS], U8)
-        nc.vector.memset(planes_in[:].bitcast(I32), 0)
+        planes_in = []
+        for w in range(2):
+            planes_w = const.tile([P, CHANNELS], U8, name="planes_in%d" % w)
+            nc.vector.memset(planes_w[:].bitcast(I32), 0)
+            planes_in.append(planes_w)
+        warm = const.tile([P, 2], F32)
+        nc.vector.memset(warm[:], 0.0)
+        nc.scalar.activation(out=warm[:, 1:2], in_=warm[:, 0:1], func=ACT.Identity)
         ident = const.tile([P, P], BF16)
         nc.vector.memset(ident[:], 0.0)
         make_identity(nc, ident[:], nomemset=True)
 
-        bias_bf = []
-        for w in range(2):
-            bias_w = const.tile([P, HALVES, PACK], BF16, name="bias_bf%d" % w)
-            nc.scalar.dma_start(out=bias_w[:], in_=bias_in[w].rearrange("(h p t) -> p h t", h=HALVES, p=P, t=PACK))
-            bias_bf.append(bias_w)
-
         x_sb = []
-        for b in range(IMAGES):
+
+        def load_image(b):
             x_b = image.tile([P, ROWS, PIXELS], BF16, name="x%d" % b)
             nc.sync.dma_start(
                 out=x_b[:].rearrange("p (g t) n -> p g (t n)", g=PASSES),
@@ -70,24 +71,47 @@ def tile_wb_pa_kernel(tc, x, Wc_words, Wc_scales, bc, W1_words, W1_scales, b1, o
             )
             x_sb.append(x_b)
 
-        for w in range(2):
+        def load_scales(w):
             for quadrant in range(QUADRANTS):
-                first = IN_QUADRANT * quadrant + PACK * PASSES * w
+                first = IN_QUADRANT * quadrant
                 nc.sync.dma_start(
-                    out=planes_in[first : first + PACK * PASSES, :].bitcast(I32),
+                    out=planes_in[w][first : first + PACK * PASSES, :].bitcast(I32),
                     in_=scales_in[w][:, PACK * quadrant : PACK * (quadrant + 1), :].bitcast(I32),
                 )
-        words_sb = []
-        for w in range(2):
-            words_w = const.tile([P, PASSES, CHANNELS], I32, name="words_in%d" % w)
-            nc.sync.dma_start(out=words_w[:], in_=words_in[w].rearrange("g p n t -> p g (n t)").bitcast(I32))
-            words_sb.append(words_w)
+
+        bias_bf = []
+
+        def load_bias(w):
+            bias_w = const.tile([P, HALVES, PACK], BF16, name="bias_bf%d" % w)
+            nc.sync.dma_start(out=bias_w[:], in_=bias_in[w].rearrange("(h p t) -> p h t", h=HALVES, p=P, t=PACK))
+            bias_bf.append(bias_w)
+
+        words_sb = [const.tile([P, HALVES, PASSES, K_PASS], I32, name="words_in%d" % w) for w in range(2)]
+
+        def load_words(w, h):
+            nc.sync.dma_start(
+                out=words_sb[w][:, h],
+                in_=words_in[w][:, :, K_PASS * h : K_PASS * (h + 1), :].rearrange("g p n t -> p g (n t)").bitcast(I32),
+            )
+
+        load_image(0)
+        load_image(1)
+        load_scales(0)
+        load_words(0, 0)
+        load_bias(0)
+        load_bias(1)
+        load_words(0, 1)
+        load_scales(1)
+        load_words(1, 0)
+        load_words(1, 1)
+        load_image(2)
+        load_image(3)
 
         averager = const.tile([P, P], BF16)
         nc.vector.tensor_scalar(out=averager[:], in0=ident[:], scalar1=1.0 / PIXELS, scalar2=None, op0=ALU.mult)
         bias = const.tile([P, 2, O_TILES], F32)
 
-        w_planes = const.tile([P, CHANNELS], U8, align_bytes=64)
+        w_planes = [const.tile([P, CHANNELS], U8, name="w_planes%d" % w, align_bytes=64) for w in range(2)]
         w_words = [
             const.tile([P, HALVES, PASSES, PACK, P], I32, name="w_words%d" % w, align_bytes=64) for w in range(2)
         ]
@@ -103,16 +127,16 @@ def tile_wb_pa_kernel(tc, x, Wc_words, Wc_scales, bc, W1_words, W1_scales, b1, o
         grouped = {}
         narrowed = {}
 
-        def permute_planes():
+        def permute_planes(w):
             nc.vector.tensor_copy(
-                out=w_planes[:].rearrange("p (h t m) -> p h m t", h=HALVES, t=PACK),
-                in_=planes_in[:].rearrange("p (h m t) -> p h m t", h=HALVES, t=PACK),
+                out=w_planes[w][:].rearrange("p (h t m) -> p h m t", h=HALVES, t=PACK),
+                in_=planes_in[w][:].rearrange("p (h m t) -> p h m t", h=HALVES, t=PACK),
             )
 
         def permute_words(w, h):
             nc.vector.tensor_copy(
                 out=w_words[w][:, h].rearrange("p g t m -> p g m t"),
-                in_=words_sb[w][:, :, K_PASS * h : K_PASS * (h + 1)].rearrange("p g (m t) -> p g m t", t=PACK),
+                in_=words_sb[w][:, h].rearrange("p g (m t) -> p g m t", t=PACK),
             )
 
         def add_pixels(b):
@@ -135,11 +159,18 @@ def tile_wb_pa_kernel(tc, x, Wc_words, Wc_scales, bc, W1_words, W1_scales, b1, o
             )
             narrowed[b] = narrower
 
-        def finish_statistics(b):
+        def finish_maximum(b):
             for halving in range(2, MAX_HALVINGS + 1):
                 halve(b, halving)
             nc.vector.tensor_reduce(out=stat[:, 1, b, :], in_=narrowed[b][:], axis=AX.X, op=ALU.max)
-            nc.vector.tensor_reduce(out=stat[:, 0, b, :], in_=sums[:, b], axis=AX.X, op=ALU.add)
+
+        def means(first, count):
+            nc.vector.tensor_reduce(
+                out=stat[:, 0, first : first + count, :].rearrange("p b r -> p (b r)"),
+                in_=sums[:, first : first + count].rearrange("p b r c -> p (b r) c"),
+                axis=AX.X,
+                op=ALU.add,
+            )
 
         def regroup(b, copy):
             grouped_b = image.tile([P, PASSES, PIXELS, PACK], BF16, name="grouped%d" % b, align_bytes=64)
@@ -157,90 +188,123 @@ def tile_wb_pa_kernel(tc, x, Wc_words, Wc_scales, bc, W1_words, W1_scales, b1, o
                 in_=grouped[b][:].rearrange("p g n t -> p (g n t)"),
             )
 
-        def invert(b):
+        def invert(first, count):
+            images = slice(first, first + count)
             nc.vector.tensor_scalar(
-                out=divisor[:, b], in0=stat[:, :, b, :], scalar1=EPS, scalar2=None, op0=ALU.add
+                out=divisor[:, images],
+                in0=stat[:, :, images, :].rearrange("p s b r -> p b s r"),
+                scalar1=EPS,
+                scalar2=None,
+                op0=ALU.add,
             )
-            nc.vector.reciprocal(out=inverse[:, b], in_=divisor[:, b])
-            nc.vector.tensor_tensor(out=offset[:, b], in0=bias[:], in1=inverse[:, b], op=ALU.mult)
+            nc.vector.reciprocal(out=inverse[:, images], in_=divisor[:, images])
+            nc.vector.tensor_tensor(
+                out=offset[:, images],
+                in0=bias[:].unsqueeze(1).to_broadcast([P, count, 2, O_TILES]),
+                in1=inverse[:, images],
+                op=ALU.mult,
+            )
 
-        def convolve(b, w, vector_banks):
-            y = result.tile([P, O_TILES, PIXELS], F32, name="y%d_%d" % (b, w))
-            out_view = outs[w][b].rearrange("(h p t) r c -> p h (t r c)", h=HALVES, p=P, t=PACK)
-            for bank in range(O_TILES // BANK_TILES):
-                acc = acc_psum.tile([P, BANK_TILES, PIXELS], F32, name="acc", tag="acc")
-                for i in range(BANK_TILES):
-                    h, t = divmod(BANK_TILES * bank + i, PACK)
-                    for g in range(PASSES):
-                        nc.tensor.matmul_mx(
-                            out=acc[:, i, :],
-                            lhsT=w_words[w][:, h, g, t, :].bitcast(FP8X4),
-                            lhsT_scale=w_planes[PACK * (PASSES * w + g) : P, K_PASS * h + P * t : K_PASS * h + P * (t + 1)],
-                            rhs=x_codes[:, b, g, :].bitcast(FP8X4),
-                            rhs_scale=x_planes[:, b, g, :],
-                            start=(g == 0),
-                            stop=(g == PASSES - 1),
-                        )
-                for i in range(BANK_TILES):
-                    j = BANK_TILES * bank + i
-                    if bank in vector_banks:
-                        nc.vector.tensor_scalar(
-                            out=y[:, j, :],
-                            in0=acc[:, i, :],
-                            scalar1=inverse[:, b, w, j : j + 1],
-                            scalar2=offset[:, b, w, j : j + 1],
-                            op0=ALU.mult,
-                            op1=ALU.add,
-                        )
-                    else:
-                        nc.scalar.activation(
-                            out=y[:, j, :],
-                            in_=acc[:, i, :],
-                            func=ACT.Identity,
-                            bias=offset[:, b, w, j : j + 1],
-                            scale=inverse[:, b, w, j : j + 1],
-                        )
-                done = BANK_TILES * (bank + 1)
-                if done % PACK == 0:
-                    h = done // PACK - 1
-                    nc.sync.dma_start(
-                        out=out_view[:, h, :], in_=y[:, PACK * h : PACK * (h + 1), :].rearrange("p t n -> p (t n)")
+        y_sb = {}
+
+        def fill_and_empty(b, w, first, count, engine):
+            if (b, w) not in y_sb:
+                y_sb[(b, w)] = result.tile([P, O_TILES, PIXELS], F32, name="y%d_%d" % (b, w))
+            y = y_sb[(b, w)]
+            acc = acc_psum.tile([P, BANK_TILES, PIXELS], F32, name="acc", tag="acc")
+            for i in range(count):
+                h, t = divmod(first + i, PACK)
+                for g in range(PASSES):
+                    nc.tensor.matmul_mx(
+                        out=acc[:, i, :],
+                        lhsT=w_words[w][:, h, g, t, :].bitcast(FP8X4),
+                        lhsT_scale=w_planes[w][PACK * g : P, K_PASS * h + P * t : K_PASS * h + P * (t + 1)],
+                        rhs=x_codes[:, b, g, :].bitcast(FP8X4),
+                        rhs_scale=x_planes[:, b, g, :],
+                        start=(g == 0),
+                        stop=(g == PASSES - 1),
+                    )
+            for i in range(count):
+                j = first + i
+                if engine == "vector":
+                    nc.vector.tensor_scalar(
+                        out=y[:, j, :],
+                        in0=acc[:, i, :],
+                        scalar1=inverse[:, b, w, j : j + 1],
+                        scalar2=offset[:, b, w, j : j + 1],
+                        op0=ALU.mult,
+                        op1=ALU.add,
+                    )
+                else:
+                    nc.scalar.activation(
+                        out=y[:, j, :],
+                        in_=acc[:, i, :],
+                        func=ACT.Identity,
+                        bias=offset[:, b, w, j : j + 1],
+                        scale=inverse[:, b, w, j : j + 1],
                     )
 
-        for b in range(IMAGES):
-            add_pixels(b)
-        regroup(0, nc.vector.tensor_copy)
+        def store(b, w, first, count):
+            h, t = divmod(first, PACK)
+            out_view = outs[w][b].rearrange("(h p t) r c -> p h t (r c)", h=HALVES, p=P, t=PACK)
+            nc.sync.dma_start(out=out_view[:, h, t : t + count, :], in_=y_sb[(b, w)][:, first : first + count, :])
+
+        def half(b, w, h, engines):
+            for i, engine in enumerate(engines):
+                fill_and_empty(b, w, PACK * h + BANK_TILES * i, BANK_TILES, engine)
+            store(b, w, PACK * h, PACK)
+
+        S, V = "scalar", "vector"
+        add_pixels(0)
+        add_pixels(1)
+        regroup(0, nc.scalar.copy)
         regroup(1, nc.scalar.copy)
-        regroup(2, nc.scalar.copy)
         halve(0, 1)
+        finish_maximum(0)
+        halve(1, 1)
+        permute_planes(0)
         quantise(0)
+        permute_words(0, 0)
+        finish_maximum(1)
+        quantise(1)
+        permute_words(0, 1)
         for w in range(2):
             nc.vector.tensor_copy(out=bias[:, w, :], in_=bias_bf[w][:].rearrange("p h t -> p (h t)"))
-        finish_statistics(0)
-        invert(0)
-        permute_planes()
-        quantise(1)
-        permute_words(0, 0)
-        permute_words(0, 1)
-        halve(1, 1)
+        means(0, 2)
+        invert(0, 2)
+        permute_planes(1)
         permute_words(1, 0)
         permute_words(1, 1)
-        convolve(0, 0, ())
-        finish_statistics(1)
-        invert(1)
-        regroup(3, nc.vector.tensor_copy)
-        convolve(0, 1, ())
-        quantise(2)
+        half(0, 0, 0, (S, S))
+        half(1, 0, 0, (S, S))
+        half(0, 0, 1, (S, S))
+        half(1, 0, 1, (V, V))
+        half(0, 1, 0, (S, S))
+        regroup(2, nc.vector.tensor_copy)
+        half(1, 1, 0, (V, V))
+        half(0, 1, 1, (S, S))
+        half(1, 1, 1, (V, S))
+        add_pixels(2)
+        add_pixels(3)
+        regroup(3, nc.scalar.copy)
         halve(2, 1)
-        convolve(1, 0, (3,))
-        finish_statistics(2)
-        invert(2)
-        quantise(3)
-        convolve(1, 1, (3,))
+        quantise(2)
+        finish_maximum(2)
+        means(2, 2)
+        invert(2, 1)
+        half(2, 0, 0, (S, S))
         halve(3, 1)
-        convolve(2, 0, (3,))
-        finish_statistics(3)
-        invert(3)
-        convolve(2, 1, (3,))
-        convolve(3, 0, (3,))
-        convolve(3, 1, (3,))
+        quantise(3)
+        half(2, 0, 1, (S, V))
+        finish_maximum(3)
+        invert(3, 1)
+        half(2, 1, 0, (S, V))
+        half(2, 1, 1, (S, V))
+        half(3, 0, 0, (S, V))
+        half(3, 0, 1, (S, V))
+        half(3, 1, 0, (S, V))
+        fill_and_empty(3, 1, 4, 2, S)
+        store(3, 1, 4, 2)
+        fill_and_empty(3, 1, 6, 1, V)
+        fill_and_empty(3, 1, 7, 1, S)
+        store(3, 1, 6, 2)

@@ -252,7 +252,7 @@ def tile_wb_pa_kernel(tc, x, Wc_words, Wc_scales, bc, W1_words, W1_scales, b1, o
         def half(b, w, h, engines):
             for i, engine in enumerate(engines):
                 fill_and_empty(b, w, PACK * h + BANK_TILES * i, BANK_TILES, engine)
-            store(b, w, PACK * h, PACK)
+                store(b, w, PACK * h + BANK_TILES * i, BANK_TILES)
 
         S, V = "scalar", "vector"
         add_pixels(0)

@@ -159,9 +159,7 @@ def tile_wb_pa_kernel(tc, x, Wc_words, Wc_scales, bc, W1_words, W1_scales, b1, o
             )
             narrowed[b] = narrower
 
-        def finish_maximum(b):
-            for halving in range(2, MAX_HALVINGS + 1):
-                halve(b, halving)
+        def top_maximum(b):
             nc.vector.tensor_reduce(out=stat[:, 1, b, :], in_=narrowed[b][:], axis=AX.X, op=ALU.max)
 
         def means(first, count):
@@ -172,14 +170,17 @@ def tile_wb_pa_kernel(tc, x, Wc_words, Wc_scales, bc, W1_words, W1_scales, b1, o
                 op=ALU.add,
             )
 
+        def regroup_pass(b, g, copy):
+            if b not in grouped:
+                grouped[b] = image.tile([P, PASSES, PIXELS, PACK], BF16, name="grouped%d" % b, align_bytes=64)
+            copy(
+                out=grouped[b][:, g].rearrange("p (c i) t -> p c t i", i=4),
+                in_=x_sb[b][:, PACK * g : PACK * (g + 1), :].rearrange("p t (c i) -> p c t i", i=4),
+            )
+
         def regroup(b, copy):
-            grouped_b = image.tile([P, PASSES, PIXELS, PACK], BF16, name="grouped%d" % b, align_bytes=64)
             for g in range(PASSES):
-                copy(
-                    out=grouped_b[:, g].rearrange("p (c i) t -> p c t i", i=4),
-                    in_=x_sb[b][:, PACK * g : PACK * (g + 1), :].rearrange("p t (c i) -> p c t i", i=4),
-                )
-            grouped[b] = grouped_b
+                regroup_pass(b, g, copy)
 
         def quantise(b):
             nc.vector.quantize_mx(
@@ -188,7 +189,7 @@ def tile_wb_pa_kernel(tc, x, Wc_words, Wc_scales, bc, W1_words, W1_scales, b1, o
                 in_=grouped[b][:].rearrange("p g n t -> p (g n t)"),
             )
 
-        def invert(first, count):
+        def add_eps(first, count):
             images = slice(first, first + count)
             nc.vector.tensor_scalar(
                 out=divisor[:, images],
@@ -197,7 +198,13 @@ def tile_wb_pa_kernel(tc, x, Wc_words, Wc_scales, bc, W1_words, W1_scales, b1, o
                 scalar2=None,
                 op0=ALU.add,
             )
+
+        def take_inverse(first, count):
+            images = slice(first, first + count)
             nc.vector.reciprocal(out=inverse[:, images], in_=divisor[:, images])
+
+        def scale_bias(first, count):
+            images = slice(first, first + count)
             nc.vector.tensor_tensor(
                 out=offset[:, images],
                 in0=bias[:].unsqueeze(1).to_broadcast([P, count, 2, O_TILES]),
@@ -249,56 +256,81 @@ def tile_wb_pa_kernel(tc, x, Wc_words, Wc_scales, bc, W1_words, W1_scales, b1, o
             out_view = outs[w][b].rearrange("(h p t) r c -> p h t (r c)", h=HALVES, p=P, t=PACK)
             nc.sync.dma_start(out=out_view[:, h, t : t + count, :], in_=y_sb[(b, w)][:, first : first + count, :])
 
+        def bank(b, w, h, i, engine):
+            fill_and_empty(b, w, PACK * h + BANK_TILES * i, BANK_TILES, engine)
+            store(b, w, PACK * h + BANK_TILES * i, BANK_TILES)
+
         def half(b, w, h, engines):
             for i, engine in enumerate(engines):
-                fill_and_empty(b, w, PACK * h + BANK_TILES * i, BANK_TILES, engine)
-                store(b, w, PACK * h + BANK_TILES * i, BANK_TILES)
+                bank(b, w, h, i, engine)
 
         S, V = "scalar", "vector"
+
+        def copy_bias(w):
+            nc.vector.tensor_copy(out=bias[:, w, :], in_=bias_bf[w][:].rearrange("p h t -> p (h t)"))
+
         add_pixels(0)
         add_pixels(1)
         regroup(0, nc.scalar.copy)
         regroup(1, nc.scalar.copy)
         halve(0, 1)
-        finish_maximum(0)
+        halve(0, 2)
         halve(1, 1)
+        halve(0, 3)
         permute_planes(0)
         quantise(0)
         permute_words(0, 0)
-        finish_maximum(1)
+        top_maximum(0)
+        halve(1, 2)
         quantise(1)
+        halve(1, 3)
         permute_words(0, 1)
-        for w in range(2):
-            nc.vector.tensor_copy(out=bias[:, w, :], in_=bias_bf[w][:].rearrange("p h t -> p (h t)"))
+        top_maximum(1)
+        copy_bias(0)
         means(0, 2)
-        invert(0, 2)
+        copy_bias(1)
+        add_eps(0, 2)
         permute_planes(1)
+        take_inverse(0, 2)
         permute_words(1, 0)
+        scale_bias(0, 2)
         permute_words(1, 1)
         half(0, 0, 0, (S, S))
         half(1, 0, 0, (S, S))
         half(0, 0, 1, (S, S))
-        half(1, 0, 1, (V, V))
+        bank(1, 0, 1, 0, V)
+        halve(2, 1)
+        bank(1, 0, 1, 1, V)
         half(0, 1, 0, (S, S))
-        regroup(2, nc.vector.tensor_copy)
-        half(1, 1, 0, (V, V))
+        regroup_pass(2, 0, nc.vector.tensor_copy)
+        halve(2, 2)
+        regroup_pass(2, 1, nc.vector.tensor_copy)
+        bank(1, 1, 0, 0, V)
+        halve(2, 3)
+        bank(1, 1, 0, 1, V)
+        halve(3, 1)
         half(0, 1, 1, (S, S))
-        half(1, 1, 1, (V, S))
+        top_maximum(2)
+        bank(1, 1, 1, 0, V)
+        halve(3, 2)
+        quantise(2)
+        bank(1, 1, 1, 1, S)
         add_pixels(2)
         add_pixels(3)
         regroup(3, nc.scalar.copy)
-        halve(2, 1)
-        quantise(2)
-        finish_maximum(2)
         means(2, 2)
-        invert(2, 1)
+        halve(3, 3)
+        add_eps(2, 1)
+        top_maximum(3)
+        take_inverse(2, 1)
+        scale_bias(2, 1)
         half(2, 0, 0, (S, S))
-        halve(3, 1)
         quantise(3)
+        add_eps(3, 1)
         half(2, 0, 1, (S, V))
-        finish_maximum(3)
-        invert(3, 1)
+        take_inverse(3, 1)
         half(2, 1, 0, (S, V))
+        scale_bias(3, 1)
         half(2, 1, 1, (S, V))
         half(3, 0, 0, (S, V))
         half(3, 0, 1, (S, V))

@@ -101,10 +101,10 @@ def tile_wb_pa_kernel(tc, x, Wc_words, Wc_scales, bc, W1_words, W1_scales, b1, o
         load_bias(0)
         load_bias(1)
         load_words(0, 1)
+        load_image(2)
         load_scales(1)
         load_words(1, 0)
         load_words(1, 1)
-        load_image(2)
         load_image(3)
 
         averager = const.tile([P, P], BF16)
@@ -271,8 +271,8 @@ def tile_wb_pa_kernel(tc, x, Wc_words, Wc_scales, bc, W1_words, W1_scales, b1, o
 
         add_pixels(0)
         add_pixels(1)
-        regroup(0, nc.scalar.copy)
-        regroup(1, nc.scalar.copy)
+        for b in range(3):
+            regroup(b, nc.scalar.copy)
         halve(0, 1)
         halve(0, 2)
         halve(1, 1)
@@ -290,10 +290,10 @@ def tile_wb_pa_kernel(tc, x, Wc_words, Wc_scales, bc, W1_words, W1_scales, b1, o
         means(0, 2)
         copy_bias(1)
         add_eps(0, 2)
-        permute_planes(1)
         take_inverse(0, 2)
-        permute_words(1, 0)
         scale_bias(0, 2)
+        permute_planes(1)
+        permute_words(1, 0)
         permute_words(1, 1)
         half(0, 0, 0, (S, S))
         half(1, 0, 0, (S, S))
@@ -302,9 +302,7 @@ def tile_wb_pa_kernel(tc, x, Wc_words, Wc_scales, bc, W1_words, W1_scales, b1, o
         halve(2, 1)
         bank(1, 0, 1, 1, V)
         half(0, 1, 0, (S, S))
-        regroup_pass(2, 0, nc.vector.tensor_copy)
         halve(2, 2)
-        regroup_pass(2, 1, nc.vector.tensor_copy)
         bank(1, 1, 0, 0, V)
         halve(2, 3)
         bank(1, 1, 0, 1, V)

@@ -298,11 +298,14 @@ def tile_wb_pa_kernel(tc, x, Wc_words, Wc_scales, bc, W1_words, W1_scales, b1, o
         half(0, 0, 0, (S, S))
         half(1, 0, 0, (S, S))
         half(0, 0, 1, (S, S))
+        add_pixels(2)
         bank(1, 0, 1, 0, V)
         halve(2, 1)
         bank(1, 0, 1, 1, V)
+        quantise(2)
         half(0, 1, 0, (S, S))
         halve(2, 2)
+        means(2, 1)
         bank(1, 1, 0, 0, V)
         halve(2, 3)
         bank(1, 1, 0, 1, V)
@@ -311,17 +314,15 @@ def tile_wb_pa_kernel(tc, x, Wc_words, Wc_scales, bc, W1_words, W1_scales, b1, o
         top_maximum(2)
         bank(1, 1, 1, 0, V)
         halve(3, 2)
-        quantise(2)
+        add_eps(2, 1)
         bank(1, 1, 1, 1, S)
-        add_pixels(2)
         add_pixels(3)
         regroup(3, nc.scalar.copy)
-        means(2, 2)
-        halve(3, 3)
-        add_eps(2, 1)
-        top_maximum(3)
         take_inverse(2, 1)
+        halve(3, 3)
         scale_bias(2, 1)
+        means(3, 1)
+        top_maximum(3)
         half(2, 0, 0, (S, S))
         quantise(3)
         add_eps(3, 1)

@@ -29,6 +29,7 @@ QUADRANTS = 4
 IN_QUADRANT = P // QUADRANTS
 SUM_CHUNK = 16
 BANK_TILES = 2
+BIAS_ROW = 16
 MAX_HALVINGS = 3
 
 FLOPS = 2 * 2 * CHANNELS * CHANNELS * IMAGES * PIXELS
@@ -46,8 +47,7 @@ def tile_wb_pa_kernel(tc, x, Wc_words, Wc_scales, bc, W1_words, W1_scales, b1, o
         const = ctx.enter_context(tc.tile_pool(name="const", bufs=1))
         image = ctx.enter_context(tc.tile_pool(name="image", bufs=1))
         result = ctx.enter_context(tc.tile_pool(name="result", bufs=1))
-        acc_psum = ctx.enter_context(tc.psum_pool(name="acc_psum", bufs=7))
-        sum_psum = ctx.enter_context(tc.psum_pool(name="sum_psum", bufs=1))
+        psum = ctx.enter_context(tc.psum_pool(name="psum", bufs=8))
 
         planes_in = []
         for w in range(2):
@@ -63,12 +63,14 @@ def tile_wb_pa_kernel(tc, x, Wc_words, Wc_scales, bc, W1_words, W1_scales, b1, o
 
         x_sb = []
 
-        def load_image(b):
+        def load_image(b, pieces=1):
             x_b = image.tile([P, ROWS, PIXELS], BF16, name="x%d" % b)
-            nc.sync.dma_start(
-                out=x_b[:].rearrange("p (g t) n -> p g (t n)", g=PASSES),
-                in_=x[b].rearrange("(g p t) h w -> p g (t h w)", g=PASSES, p=P, t=PACK),
-            )
+            width = PASSES // pieces
+            for g in range(0, PASSES, width):
+                nc.sync.dma_start(
+                    out=x_b[:, PACK * g : PACK * (g + width), :].rearrange("p (g t) n -> p g (t n)", g=width),
+                    in_=x[b].rearrange("(g p t) h w -> p g (t h w)", g=PASSES, p=P, t=PACK)[:, g : g + width],
+                )
             x_sb.append(x_b)
 
         def load_scales(w):
@@ -79,12 +81,13 @@ def tile_wb_pa_kernel(tc, x, Wc_words, Wc_scales, bc, W1_words, W1_scales, b1, o
                     in_=scales_in[w][:, PACK * quadrant : PACK * (quadrant + 1), :].bitcast(I32),
                 )
 
-        bias_bf = []
+        bias_bf = const.tile([P, 2, BIAS_ROW], BF16)
 
         def load_bias(w):
-            bias_w = const.tile([P, HALVES, PACK], BF16, name="bias_bf%d" % w)
-            nc.sync.dma_start(out=bias_w[:], in_=bias_in[w].rearrange("(h p t) -> p h t", h=HALVES, p=P, t=PACK))
-            bias_bf.append(bias_w)
+            nc.sync.dma_start(
+                out=bias_bf[:, w, 0:O_TILES].rearrange("p (h t) -> p h t", h=HALVES),
+                in_=bias_in[w].rearrange("(h p t) -> p h t", h=HALVES, p=P, t=PACK),
+            )
 
         words_sb = [const.tile([P, HALVES, PASSES, K_PASS], I32, name="words_in%d" % w) for w in range(2)]
 
@@ -94,10 +97,10 @@ def tile_wb_pa_kernel(tc, x, Wc_words, Wc_scales, bc, W1_words, W1_scales, b1, o
                 in_=words_in[w][:, :, K_PASS * h : K_PASS * (h + 1), :].rearrange("g p n t -> p g (n t)").bitcast(I32),
             )
 
-        load_image(0)
-        load_image(1)
+        load_image(0, 2)
         load_scales(0)
         load_words(0, 0)
+        load_image(1)
         load_bias(0)
         load_bias(1)
         load_words(0, 1)
@@ -109,7 +112,6 @@ def tile_wb_pa_kernel(tc, x, Wc_words, Wc_scales, bc, W1_words, W1_scales, b1, o
 
         averager = const.tile([P, P], BF16)
         nc.vector.tensor_scalar(out=averager[:], in0=ident[:], scalar1=1.0 / PIXELS, scalar2=None, op0=ALU.mult)
-        bias = const.tile([P, 2, O_TILES], F32)
 
         w_planes = [const.tile([P, CHANNELS], U8, name="w_planes%d" % w, align_bytes=64) for w in range(2)]
         w_words = [
@@ -117,15 +119,15 @@ def tile_wb_pa_kernel(tc, x, Wc_words, Wc_scales, bc, W1_words, W1_scales, b1, o
         ]
 
         stat = const.tile([P, 2, IMAGES, ROWS], F32)
-        sums = sum_psum.tile([P, IMAGES, ROWS, SUM_CHUNK], F32)
         x_codes = const.tile([P, IMAGES, PASSES, PIXELS], U32, align_bytes=64)
         x_planes = const.tile([P, IMAGES, PASSES, PIXELS], U8, align_bytes=64)
-        divisor = const.tile([P, IMAGES, 2, O_TILES], F32)
-        inverse = const.tile([P, IMAGES, 2, O_TILES], F32)
-        offset = const.tile([P, IMAGES, 2, O_TILES], F32)
+        divisor = const.tile([P, 2, IMAGES, O_TILES], F32)
+        inverse = const.tile([P, 2, IMAGES, O_TILES], F32)
+        offset = const.tile([P, 2, IMAGES, O_TILES], F32)
 
         grouped = {}
         narrowed = {}
+        sums = {}
 
         def permute_planes(w):
             nc.vector.tensor_copy(
@@ -140,10 +142,11 @@ def tile_wb_pa_kernel(tc, x, Wc_words, Wc_scales, bc, W1_words, W1_scales, b1, o
             )
 
         def add_pixels(b):
+            sums[b] = psum.tile([P, ROWS, SUM_CHUNK], F32, name="sums", tag="bank")
             chunks = PIXELS // SUM_CHUNK
             for c in range(chunks):
                 nc.tensor.matmul(
-                    out=sums[:, b],
+                    out=sums[b][:],
                     lhsT=averager[:],
                     rhs=x_sb[b][:, :, SUM_CHUNK * c : SUM_CHUNK * (c + 1)],
                     start=(c == 0),
@@ -162,13 +165,8 @@ def tile_wb_pa_kernel(tc, x, Wc_words, Wc_scales, bc, W1_words, W1_scales, b1, o
         def top_maximum(b):
             nc.vector.tensor_reduce(out=stat[:, 1, b, :], in_=narrowed[b][:], axis=AX.X, op=ALU.max)
 
-        def means(first, count):
-            nc.vector.tensor_reduce(
-                out=stat[:, 0, first : first + count, :].rearrange("p b r -> p (b r)"),
-                in_=sums[:, first : first + count].rearrange("p b r c -> p (b r) c"),
-                axis=AX.X,
-                op=ALU.add,
-            )
+        def means(b):
+            nc.vector.tensor_reduce(out=stat[:, 0, b, :], in_=sums[b][:], axis=AX.X, op=ALU.add)
 
         def regroup_pass(b, g, copy):
             if b not in grouped:
@@ -189,26 +187,29 @@ def tile_wb_pa_kernel(tc, x, Wc_words, Wc_scales, bc, W1_words, W1_scales, b1, o
                 in_=grouped[b][:].rearrange("p g n t -> p (g n t)"),
             )
 
-        def add_eps(first, count):
-            images = slice(first, first + count)
-            nc.vector.tensor_scalar(
-                out=divisor[:, images],
-                in0=stat[:, :, images, :].rearrange("p s b r -> p b s r"),
-                scalar1=EPS,
-                scalar2=None,
-                op0=ALU.add,
+        def quantise_pass(b, g):
+            nc.vector.quantize_mx(
+                out=x_codes[:, b, g].bitcast(FP8X4),
+                scales=x_planes[:, b, g],
+                in_=grouped[b][:, g].rearrange("p n t -> p (n t)"),
             )
 
-        def take_inverse(first, count):
+        def add_eps(w, first, count):
             images = slice(first, first + count)
-            nc.vector.reciprocal(out=inverse[:, images], in_=divisor[:, images])
+            nc.vector.tensor_scalar(
+                out=divisor[:, w, images], in0=stat[:, w, images], scalar1=EPS, scalar2=None, op0=ALU.add
+            )
 
-        def scale_bias(first, count):
+        def take_inverse(w, first, count):
+            images = slice(first, first + count)
+            nc.vector.reciprocal(out=inverse[:, w, images], in_=divisor[:, w, images])
+
+        def scale_bias(w, first, count):
             images = slice(first, first + count)
             nc.vector.tensor_tensor(
-                out=offset[:, images],
-                in0=bias[:].unsqueeze(1).to_broadcast([P, count, 2, O_TILES]),
-                in1=inverse[:, images],
+                out=offset[:, w, images],
+                in0=bias_bf[:, w : w + 1, 0:O_TILES].to_broadcast([P, count, O_TILES]),
+                in1=inverse[:, w, images],
                 op=ALU.mult,
             )
 
@@ -218,7 +219,7 @@ def tile_wb_pa_kernel(tc, x, Wc_words, Wc_scales, bc, W1_words, W1_scales, b1, o
             if (b, w) not in y_sb:
                 y_sb[(b, w)] = result.tile([P, O_TILES, PIXELS], F32, name="y%d_%d" % (b, w))
             y = y_sb[(b, w)]
-            acc = acc_psum.tile([P, BANK_TILES, PIXELS], F32, name="acc", tag="acc")
+            acc = psum.tile([P, BANK_TILES, PIXELS], F32, name="acc", tag="bank")
             for i in range(count):
                 h, t = divmod(first + i, PACK)
                 for g in range(PASSES):
@@ -237,8 +238,8 @@ def tile_wb_pa_kernel(tc, x, Wc_words, Wc_scales, bc, W1_words, W1_scales, b1, o
                     nc.vector.tensor_scalar(
                         out=y[:, j, :],
                         in0=acc[:, i, :],
-                        scalar1=inverse[:, b, w, j : j + 1],
-                        scalar2=offset[:, b, w, j : j + 1],
+                        scalar1=inverse[:, w, b, j : j + 1],
+                        scalar2=offset[:, w, b, j : j + 1],
                         op0=ALU.mult,
                         op1=ALU.add,
                     )
@@ -247,8 +248,8 @@ def tile_wb_pa_kernel(tc, x, Wc_words, Wc_scales, bc, W1_words, W1_scales, b1, o
                         out=y[:, j, :],
                         in_=acc[:, i, :],
                         func=ACT.Identity,
-                        bias=offset[:, b, w, j : j + 1],
-                        scale=inverse[:, b, w, j : j + 1],
+                        bias=offset[:, w, b, j : j + 1],
+                        scale=inverse[:, w, b, j : j + 1],
                     )
 
         def store(b, w, first, count):
@@ -266,70 +267,80 @@ def tile_wb_pa_kernel(tc, x, Wc_words, Wc_scales, bc, W1_words, W1_scales, b1, o
 
         S, V = "scalar", "vector"
 
-        def copy_bias(w):
-            nc.vector.tensor_copy(out=bias[:, w, :], in_=bias_bf[w][:].rearrange("p h t -> p (h t)"))
-
         add_pixels(0)
-        add_pixels(1)
-        for b in range(3):
-            regroup(b, nc.scalar.copy)
+        regroup(0, nc.scalar.copy)
         halve(0, 1)
-        halve(0, 2)
-        halve(1, 1)
-        halve(0, 3)
         permute_planes(0)
-        quantise(0)
+        halve(0, 2)
         permute_words(0, 0)
-        top_maximum(0)
+        quantise(0)
+        halve(0, 3)
+        means(0)
+        regroup(1, nc.scalar.copy)
+        add_eps(0, 0, 1)
+        halve(1, 1)
+        take_inverse(0, 0, 1)
+        permute_words(0, 1)
+        scale_bias(0, 0, 1)
+        half(0, 0, 0, (S, S))
+        add_pixels(1)
+        half(0, 0, 1, (S, S))
         halve(1, 2)
         quantise(1)
+        means(1)
         halve(1, 3)
-        permute_words(0, 1)
+        add_eps(0, 1, 1)
+        top_maximum(0)
+        take_inverse(0, 1, 1)
         top_maximum(1)
-        copy_bias(0)
-        means(0, 2)
-        copy_bias(1)
-        add_eps(0, 2)
-        take_inverse(0, 2)
-        scale_bias(0, 2)
-        permute_planes(1)
-        permute_words(1, 0)
-        permute_words(1, 1)
-        half(0, 0, 0, (S, S))
+        scale_bias(0, 1, 1)
         half(1, 0, 0, (S, S))
-        half(0, 0, 1, (S, S))
-        add_pixels(2)
+        permute_planes(1)
+        add_eps(1, 0, 2)
+        permute_words(1, 0)
+        take_inverse(1, 0, 2)
+        regroup_pass(2, 0, nc.scalar.copy)
+        permute_words(1, 1)
+        scale_bias(1, 0, 2)
         bank(1, 0, 1, 0, V)
         halve(2, 1)
-        bank(1, 0, 1, 1, V)
-        quantise(2)
-        half(0, 1, 0, (S, S))
+        bank(1, 0, 1, 1, S)
+        add_pixels(2)
+        regroup_pass(2, 1, nc.scalar.copy)
+        bank(0, 1, 0, 0, V)
         halve(2, 2)
-        means(2, 1)
-        bank(1, 1, 0, 0, V)
+        means(2)
+        bank(0, 1, 0, 1, S)
+        quantise(2)
         halve(2, 3)
+        add_eps(0, 2, 1)
+        bank(1, 1, 0, 0, S)
+        top_maximum(2)
+        take_inverse(0, 2, 1)
         bank(1, 1, 0, 1, V)
         halve(3, 1)
-        half(0, 1, 1, (S, S))
-        top_maximum(2)
-        bank(1, 1, 1, 0, V)
+        scale_bias(0, 2, 1)
+        bank(0, 1, 1, 0, S)
+        regroup_pass(3, 0, nc.scalar.copy)
         halve(3, 2)
-        add_eps(2, 1)
-        bank(1, 1, 1, 1, S)
-        add_pixels(3)
-        regroup(3, nc.scalar.copy)
-        take_inverse(2, 1)
+        bank(0, 1, 1, 1, V)
         halve(3, 3)
-        scale_bias(2, 1)
-        means(3, 1)
+        bank(1, 1, 1, 0, S)
+        regroup_pass(3, 1, nc.scalar.copy)
+        bank(1, 1, 1, 1, V)
+        add_pixels(3)
         top_maximum(3)
         half(2, 0, 0, (S, S))
+        means(3)
+        add_eps(1, 2, 2)
         quantise(3)
-        add_eps(3, 1)
+        take_inverse(1, 2, 2)
+        add_eps(0, 3, 1)
+        scale_bias(1, 2, 2)
+        take_inverse(0, 3, 1)
         half(2, 0, 1, (S, V))
-        take_inverse(3, 1)
+        scale_bias(0, 3, 1)
         half(2, 1, 0, (S, V))
-        scale_bias(3, 1)
         half(2, 1, 1, (S, V))
         half(3, 0, 0, (S, V))
         half(3, 0, 1, (S, V))

@@ -168,6 +168,13 @@ def tile_wb_pa_kernel(tc, x, Wc_words, Wc_scales, bc, W1_words, W1_scales, b1, o
         def means(b):
             nc.vector.tensor_reduce(out=stat[:, 0, b, :], in_=sums[b][:], axis=AX.X, op=ALU.add)
 
+        def means_on_vector(b):
+            total = const.tile([P, ROWS], F32, name="total%d" % b)
+            nc.vector.tensor_reduce(out=total[:], in_=x_sb[b][:], axis=AX.X, op=ALU.add)
+            nc.vector.tensor_scalar(
+                out=divisor[:, 0, b], in0=total[:], scalar1=1.0 / PIXELS, scalar2=EPS, op0=ALU.mult, op1=ALU.add
+            )
+
         def regroup_pass(b, g, copy):
             if b not in grouped:
                 grouped[b] = image.tile([P, PASSES, PIXELS, PACK], BF16, name="grouped%d" % b, align_bytes=64)
@@ -299,52 +306,47 @@ def tile_wb_pa_kernel(tc, x, Wc_words, Wc_scales, bc, W1_words, W1_scales, b1, o
         add_eps(1, 0, 2)
         permute_words(1, 0)
         take_inverse(1, 0, 2)
-        regroup_pass(2, 0, nc.scalar.copy)
-        permute_words(1, 1)
-        scale_bias(1, 0, 2)
-        bank(1, 0, 1, 0, V)
-        halve(2, 1)
-        bank(1, 0, 1, 1, S)
+        half(1, 0, 1, (S, S))
         add_pixels(2)
-        regroup_pass(2, 1, nc.scalar.copy)
-        bank(0, 1, 0, 0, V)
-        halve(2, 2)
-        means(2)
-        bank(0, 1, 0, 1, S)
+        regroup(2, nc.vector.tensor_copy)
+        scale_bias(1, 0, 2)
+        permute_words(1, 1)
+        half(0, 1, 0, (S, S))
+        halve(2, 1)
         quantise(2)
-        halve(2, 3)
+        means(2)
+        half(1, 1, 0, (S, S))
+        halve(2, 2)
         add_eps(0, 2, 1)
-        bank(1, 1, 0, 0, S)
-        top_maximum(2)
+        halve(2, 3)
         take_inverse(0, 2, 1)
-        bank(1, 1, 0, 1, V)
-        halve(3, 1)
+        half(0, 1, 1, (S, S))
+        top_maximum(2)
         scale_bias(0, 2, 1)
-        bank(0, 1, 1, 0, S)
-        regroup_pass(3, 0, nc.scalar.copy)
-        halve(3, 2)
-        bank(0, 1, 1, 1, V)
-        halve(3, 3)
-        bank(1, 1, 1, 0, S)
-        regroup_pass(3, 1, nc.scalar.copy)
-        bank(1, 1, 1, 1, V)
-        add_pixels(3)
-        top_maximum(3)
-        half(2, 0, 0, (S, S))
-        means(3)
-        add_eps(1, 2, 2)
+        regroup_pass(3, 0, nc.vector.tensor_copy)
+        add_eps(1, 2, 1)
+        half(1, 1, 1, (S, S))
+        regroup_pass(3, 1, nc.vector.tensor_copy)
+        take_inverse(1, 2, 1)
+        halve(3, 1)
+        scale_bias(1, 2, 1)
         quantise(3)
-        take_inverse(1, 2, 2)
-        add_eps(0, 3, 1)
-        scale_bias(1, 2, 2)
+        half(2, 0, 0, (S, S))
+        means_on_vector(3)
+        half(2, 0, 1, (S, S))
+        halve(3, 2)
         take_inverse(0, 3, 1)
-        half(2, 0, 1, (S, V))
+        halve(3, 3)
         scale_bias(0, 3, 1)
-        half(2, 1, 0, (S, V))
+        half(2, 1, 0, (S, S))
+        top_maximum(3)
         half(2, 1, 1, (S, V))
+        add_eps(1, 3, 1)
         half(3, 0, 0, (S, V))
+        take_inverse(1, 3, 1)
         half(3, 0, 1, (S, V))
-        half(3, 1, 0, (S, V))
+        scale_bias(1, 3, 1)
+        half(3, 1, 0, (V, S))
         fill_and_empty(3, 1, 4, 2, S)
         store(3, 1, 4, 2)
         fill_and_empty(3, 1, 6, 1, V)

@@ -99,12 +99,12 @@ def tile_wb_pa_kernel(tc, x, Wc_words, Wc_scales, bc, W1_words, W1_scales, b1, o
 
         load_image(0, 2)
         load_scales(0)
-        load_words(0, 0)
         load_image(1)
+        load_words(0, 0)
         load_bias(0)
-        load_bias(1)
         load_words(0, 1)
         load_image(2)
+        load_bias(1)
         load_scales(1)
         load_words(1, 0)
         load_words(1, 1)
@@ -171,7 +171,7 @@ def tile_wb_pa_kernel(tc, x, Wc_words, Wc_scales, bc, W1_words, W1_scales, b1, o
         def means_on_vector(b):
             total = const.tile([P, ROWS], F32, name="total%d" % b)
             nc.vector.tensor_reduce(out=total[:], in_=x_sb[b][:], axis=AX.X, op=ALU.add)
-            nc.vector.tensor_scalar(
+            nc.gpsimd.tensor_scalar(
                 out=divisor[:, 0, b], in0=total[:], scalar1=1.0 / PIXELS, scalar2=EPS, op0=ALU.mult, op1=ALU.add
             )
 
@@ -203,8 +203,13 @@ def tile_wb_pa_kernel(tc, x, Wc_words, Wc_scales, bc, W1_words, W1_scales, b1, o
 
         def add_eps(w, first, count):
             images = slice(first, first + count)
-            nc.vector.tensor_scalar(
-                out=divisor[:, w, images], in0=stat[:, w, images], scalar1=EPS, scalar2=None, op0=ALU.add
+            nc.gpsimd.tensor_scalar(
+                out=divisor[:, w, images],
+                in0=stat[:, w, images],
+                scalar1=EPS,
+                scalar2=1.0,
+                op0=ALU.add,
+                op1=ALU.mult,
             )
 
         def take_inverse(w, first, count):
@@ -213,7 +218,7 @@ def tile_wb_pa_kernel(tc, x, Wc_words, Wc_scales, bc, W1_words, W1_scales, b1, o
 
         def scale_bias(w, first, count):
             images = slice(first, first + count)
-            nc.vector.tensor_tensor(
+            nc.gpsimd.tensor_tensor(
                 out=offset[:, w, images],
                 in0=bias_bf[:, w : w + 1, 0:O_TILES].to_broadcast([P, count, O_TILES]),
                 in1=inverse[:, w, images],
@@ -275,24 +280,24 @@ def tile_wb_pa_kernel(tc, x, Wc_words, Wc_scales, bc, W1_words, W1_scales, b1, o
         S, V = "scalar", "vector"
 
         add_pixels(0)
+        add_pixels(1)
         regroup(0, nc.scalar.copy)
+        regroup(1, nc.scalar.copy)
         halve(0, 1)
         permute_planes(0)
         halve(0, 2)
-        permute_words(0, 0)
-        quantise(0)
-        halve(0, 3)
-        means(0)
-        regroup(1, nc.scalar.copy)
-        add_eps(0, 0, 1)
         halve(1, 1)
-        take_inverse(0, 0, 1)
+        quantise(0)
+        permute_words(0, 0)
+        means(0)
+        halve(0, 3)
+        add_eps(0, 0, 1)
         permute_words(0, 1)
+        take_inverse(0, 0, 1)
+        halve(1, 2)
         scale_bias(0, 0, 1)
         half(0, 0, 0, (S, S))
-        add_pixels(1)
         half(0, 0, 1, (S, S))
-        halve(1, 2)
         quantise(1)
         means(1)
         halve(1, 3)
@@ -302,51 +307,53 @@ def tile_wb_pa_kernel(tc, x, Wc_words, Wc_scales, bc, W1_words, W1_scales, b1, o
         top_maximum(1)
         scale_bias(0, 1, 1)
         half(1, 0, 0, (S, S))
-        permute_planes(1)
         add_eps(1, 0, 2)
-        permute_words(1, 0)
+        regroup(2, nc.vector.tensor_copy)
+        permute_planes(1)
         take_inverse(1, 0, 2)
+        permute_words(1, 0)
+        scale_bias(1, 0, 2)
         half(1, 0, 1, (S, S))
         add_pixels(2)
-        regroup(2, nc.vector.tensor_copy)
-        scale_bias(1, 0, 2)
         permute_words(1, 1)
         half(0, 1, 0, (S, S))
         halve(2, 1)
         quantise(2)
-        means(2)
         half(1, 1, 0, (S, S))
         halve(2, 2)
-        add_eps(0, 2, 1)
-        halve(2, 3)
-        take_inverse(0, 2, 1)
-        half(0, 1, 1, (S, S))
-        top_maximum(2)
-        scale_bias(0, 2, 1)
         regroup_pass(3, 0, nc.vector.tensor_copy)
+        halve(2, 3)
+        half(0, 1, 1, (S, S))
+        means(2)
+        add_eps(0, 2, 1)
+        halve(3, 1)
+        top_maximum(2)
         add_eps(1, 2, 1)
-        half(1, 1, 1, (S, S))
+        take_inverse(0, 2, 1)
+        scale_bias(0, 2, 1)
         regroup_pass(3, 1, nc.vector.tensor_copy)
         take_inverse(1, 2, 1)
-        halve(3, 1)
         scale_bias(1, 2, 1)
-        quantise(3)
-        half(2, 0, 0, (S, S))
-        means_on_vector(3)
-        half(2, 0, 1, (S, S))
+        bank(1, 1, 1, 0, S)
+        bank(1, 1, 1, 1, V)
         halve(3, 2)
-        take_inverse(0, 3, 1)
+        half(2, 0, 0, (S, S))
+        quantise(3)
         halve(3, 3)
-        scale_bias(0, 3, 1)
-        half(2, 1, 0, (S, S))
+        half(2, 0, 1, (S, S))
+        means_on_vector(3)
         top_maximum(3)
-        half(2, 1, 1, (S, V))
         add_eps(1, 3, 1)
-        half(3, 0, 0, (S, V))
+        bank(2, 1, 0, 0, S)
+        bank(2, 1, 0, 1, V)
+        take_inverse(0, 3, 1)
+        scale_bias(0, 3, 1)
         take_inverse(1, 3, 1)
-        half(3, 0, 1, (S, V))
         scale_bias(1, 3, 1)
-        half(3, 1, 0, (V, S))
+        half(2, 1, 1, (S, V))
+        half(3, 0, 0, (S, V))
+        half(3, 0, 1, (S, V))
+        half(3, 1, 0, (S, V))
         fill_and_empty(3, 1, 4, 2, S)
         store(3, 1, 4, 2)
         fill_and_empty(3, 1, 6, 1, V)

@@ -168,11 +168,17 @@ def tile_wb_pa_kernel(tc, x, Wc_words, Wc_scales, bc, W1_words, W1_scales, b1, o
         def means(b):
             nc.vector.tensor_reduce(out=stat[:, 0, b, :], in_=sums[b][:], axis=AX.X, op=ALU.add)
 
-        def means_on_vector(b):
-            total = const.tile([P, ROWS], F32, name="total%d" % b)
-            nc.vector.tensor_reduce(out=total[:], in_=x_sb[b][:], axis=AX.X, op=ALU.add)
-            nc.gpsimd.tensor_scalar(
-                out=divisor[:, 0, b], in0=total[:], scalar1=1.0 / PIXELS, scalar2=EPS, op0=ALU.mult, op1=ALU.add
+        def sum_on_vector(b):
+            nc.vector.tensor_reduce(out=stat[:, 0, b, :], in_=x_sb[b][:], axis=AX.X, op=ALU.add)
+
+        def mean_divisor(b):
+            nc.vector.tensor_scalar(
+                out=divisor[:, 0, b],
+                in0=stat[:, 0, b, :],
+                scalar1=1.0 / PIXELS,
+                scalar2=EPS,
+                op0=ALU.mult,
+                op1=ALU.add,
             )
 
         def regroup_pass(b, g, copy):
@@ -203,13 +209,8 @@ def tile_wb_pa_kernel(tc, x, Wc_words, Wc_scales, bc, W1_words, W1_scales, b1, o
 
         def add_eps(w, first, count):
             images = slice(first, first + count)
-            nc.gpsimd.tensor_scalar(
-                out=divisor[:, w, images],
-                in0=stat[:, w, images],
-                scalar1=EPS,
-                scalar2=1.0,
-                op0=ALU.add,
-                op1=ALU.mult,
+            nc.vector.tensor_scalar(
+                out=divisor[:, w, images], in0=stat[:, w, images], scalar1=EPS, scalar2=None, op0=ALU.add
             )
 
         def take_inverse(w, first, count):
@@ -218,7 +219,7 @@ def tile_wb_pa_kernel(tc, x, Wc_words, Wc_scales, bc, W1_words, W1_scales, b1, o
 
         def scale_bias(w, first, count):
             images = slice(first, first + count)
-            nc.gpsimd.tensor_tensor(
+            nc.vector.tensor_tensor(
                 out=offset[:, w, images],
                 in0=bias_bf[:, w : w + 1, 0:O_TILES].to_broadcast([P, count, O_TILES]),
                 in1=inverse[:, w, images],
@@ -226,13 +227,19 @@ def tile_wb_pa_kernel(tc, x, Wc_words, Wc_scales, bc, W1_words, W1_scales, b1, o
             )
 
         y_sb = {}
+        products = {}
 
         def fill_and_empty(b, w, first, count, engine):
+            fill(b, w, first, count)
+            for i in range(count):
+                empty(b, w, first + i, engine)
+
+        def fill(b, w, first, count):
             if (b, w) not in y_sb:
                 y_sb[(b, w)] = result.tile([P, O_TILES, PIXELS], F32, name="y%d_%d" % (b, w))
-            y = y_sb[(b, w)]
             acc = psum.tile([P, BANK_TILES, PIXELS], F32, name="acc", tag="bank")
             for i in range(count):
+                products[(b, w, first + i)] = acc[:, i, :]
                 h, t = divmod(first + i, PACK)
                 for g in range(PASSES):
                     nc.tensor.matmul_mx(
@@ -244,25 +251,26 @@ def tile_wb_pa_kernel(tc, x, Wc_words, Wc_scales, bc, W1_words, W1_scales, b1, o
                         start=(g == 0),
                         stop=(g == PASSES - 1),
                     )
-            for i in range(count):
-                j = first + i
-                if engine == "vector":
-                    nc.vector.tensor_scalar(
-                        out=y[:, j, :],
-                        in0=acc[:, i, :],
-                        scalar1=inverse[:, w, b, j : j + 1],
-                        scalar2=offset[:, w, b, j : j + 1],
-                        op0=ALU.mult,
-                        op1=ALU.add,
-                    )
-                else:
-                    nc.scalar.activation(
-                        out=y[:, j, :],
-                        in_=acc[:, i, :],
-                        func=ACT.Identity,
-                        bias=offset[:, w, b, j : j + 1],
-                        scale=inverse[:, w, b, j : j + 1],
-                    )
+
+        def empty(b, w, j, engine):
+            y = y_sb[(b, w)]
+            if engine == "vector":
+                nc.vector.tensor_scalar(
+                    out=y[:, j, :],
+                    in0=products[(b, w, j)],
+                    scalar1=inverse[:, w, b, j : j + 1],
+                    scalar2=offset[:, w, b, j : j + 1],
+                    op0=ALU.mult,
+                    op1=ALU.add,
+                )
+            else:
+                nc.scalar.activation(
+                    out=y[:, j, :],
+                    in_=products[(b, w, j)],
+                    func=ACT.Identity,
+                    bias=offset[:, w, b, j : j + 1],
+                    scale=inverse[:, w, b, j : j + 1],
+                )
 
         def store(b, w, first, count):
             h, t = divmod(first, PACK)
@@ -325,32 +333,38 @@ def tile_wb_pa_kernel(tc, x, Wc_words, Wc_scales, bc, W1_words, W1_scales, b1, o
         halve(2, 3)
         half(0, 1, 1, (S, S))
         means(2)
-        add_eps(0, 2, 1)
         halve(3, 1)
+        add_eps(0, 2, 1)
         top_maximum(2)
-        add_eps(1, 2, 1)
         take_inverse(0, 2, 1)
-        scale_bias(0, 2, 1)
         regroup_pass(3, 1, nc.vector.tensor_copy)
-        take_inverse(1, 2, 1)
-        scale_bias(1, 2, 1)
-        bank(1, 1, 1, 0, S)
-        bank(1, 1, 1, 1, V)
+        scale_bias(0, 2, 1)
+        add_eps(1, 2, 1)
+        half(1, 1, 1, (S, S))
         halve(3, 2)
-        half(2, 0, 0, (S, S))
+        take_inverse(1, 2, 1)
         quantise(3)
+        scale_bias(1, 2, 1)
+        half(2, 0, 0, (S, S))
         halve(3, 3)
         half(2, 0, 1, (S, S))
-        means_on_vector(3)
+        sum_on_vector(3)
         top_maximum(3)
+        mean_divisor(3)
+        fill(2, 1, 0, 2)
+        empty(2, 1, 0, V)
         add_eps(1, 3, 1)
-        bank(2, 1, 0, 0, S)
-        bank(2, 1, 0, 1, V)
         take_inverse(0, 3, 1)
-        scale_bias(0, 3, 1)
+        empty(2, 1, 1, V)
+        store(2, 1, 0, 2)
         take_inverse(1, 3, 1)
+        scale_bias(0, 3, 1)
+        fill(2, 1, 2, 2)
+        empty(2, 1, 2, V)
         scale_bias(1, 3, 1)
-        half(2, 1, 1, (S, V))
+        empty(2, 1, 3, V)
+        store(2, 1, 2, 2)
+        half(2, 1, 1, (S, S))
         half(3, 0, 0, (S, V))
         half(3, 0, 1, (S, V))
         half(3, 1, 0, (S, V))

@@ -285,6 +285,11 @@ def tile_wb_pa_kernel(tc, x, Wc_words, Wc_scales, bc, W1_words, W1_scales, b1, o
             for i, engine in enumerate(engines):
                 bank(b, w, h, i, engine)
 
+        def whole_half(b, w, h, engines):
+            for i, engine in enumerate(engines):
+                fill_and_empty(b, w, PACK * h + BANK_TILES * i, BANK_TILES, engine)
+            store(b, w, PACK * h, PACK)
+
         S, V = "scalar", "vector"
 
         add_pixels(0)
@@ -304,8 +309,8 @@ def tile_wb_pa_kernel(tc, x, Wc_words, Wc_scales, bc, W1_words, W1_scales, b1, o
         take_inverse(0, 0, 1)
         halve(1, 2)
         scale_bias(0, 0, 1)
-        half(0, 0, 0, (S, S))
-        half(0, 0, 1, (S, S))
+        whole_half(0, 0, 0, (S, S))
+        whole_half(0, 0, 1, (S, S))
         quantise(1)
         means(1)
         halve(1, 3)
@@ -314,24 +319,24 @@ def tile_wb_pa_kernel(tc, x, Wc_words, Wc_scales, bc, W1_words, W1_scales, b1, o
         take_inverse(0, 1, 1)
         top_maximum(1)
         scale_bias(0, 1, 1)
-        half(1, 0, 0, (S, S))
+        whole_half(1, 0, 0, (S, S))
         add_eps(1, 0, 2)
         regroup(2, nc.vector.tensor_copy)
         permute_planes(1)
         take_inverse(1, 0, 2)
         permute_words(1, 0)
         scale_bias(1, 0, 2)
-        half(1, 0, 1, (S, S))
+        whole_half(1, 0, 1, (S, S))
         add_pixels(2)
         permute_words(1, 1)
-        half(0, 1, 0, (S, S))
+        whole_half(0, 1, 0, (S, S))
         halve(2, 1)
         quantise(2)
-        half(1, 1, 0, (S, S))
+        whole_half(1, 1, 0, (S, S))
         halve(2, 2)
         regroup_pass(3, 0, nc.vector.tensor_copy)
         halve(2, 3)
-        half(0, 1, 1, (S, S))
+        whole_half(0, 1, 1, (S, S))
         means(2)
         halve(3, 1)
         add_eps(0, 2, 1)
@@ -340,14 +345,14 @@ def tile_wb_pa_kernel(tc, x, Wc_words, Wc_scales, bc, W1_words, W1_scales, b1, o
         regroup_pass(3, 1, nc.vector.tensor_copy)
         scale_bias(0, 2, 1)
         add_eps(1, 2, 1)
-        half(1, 1, 1, (S, S))
+        whole_half(1, 1, 1, (S, S))
         halve(3, 2)
         take_inverse(1, 2, 1)
         quantise(3)
         scale_bias(1, 2, 1)
-        half(2, 0, 0, (S, S))
+        whole_half(2, 0, 0, (S, S))
         halve(3, 3)
-        half(2, 0, 1, (S, S))
+        whole_half(2, 0, 1, (S, S))
         sum_on_vector(3)
         top_maximum(3)
         mean_divisor(3)

@@ -97,12 +97,19 @@ def tile_wb_pa_kernel(tc, x, Wc_words, Wc_scales, bc, W1_words, W1_scales, b1, o
                 in_=words_in[w][:, :, K_PASS * h : K_PASS * (h + 1), :].rearrange("g p n t -> p g (n t)").bitcast(I32),
             )
 
+        def load_words_pass(w, h, g):
+            nc.sync.dma_start(
+                out=words_sb[w][:, h, g],
+                in_=words_in[w][g, :, K_PASS * h : K_PASS * (h + 1), :].rearrange("p n t -> p (n t)").bitcast(I32),
+            )
+
         load_image(0, 2)
         load_scales(0)
         load_image(1)
-        load_words(0, 0)
-        load_bias(0)
+        load_words_pass(0, 0, 0)
+        load_words_pass(0, 0, 1)
         load_words(0, 1)
+        load_bias(0)
         load_image(2)
         load_bias(1)
         load_scales(1)
@@ -139,6 +146,12 @@ def tile_wb_pa_kernel(tc, x, Wc_words, Wc_scales, bc, W1_words, W1_scales, b1, o
             nc.vector.tensor_copy(
                 out=w_words[w][:, h].rearrange("p g t m -> p g m t"),
                 in_=words_sb[w][:, h].rearrange("p g (m t) -> p g m t", t=PACK),
+            )
+
+        def permute_words_pass(w, h, g):
+            nc.vector.tensor_copy(
+                out=w_words[w][:, h, g].rearrange("p t m -> p m t"),
+                in_=words_sb[w][:, h, g].rearrange("p (m t) -> p m t", t=PACK),
             )
 
         def add_pixels(b):
@@ -298,17 +311,19 @@ def tile_wb_pa_kernel(tc, x, Wc_words, Wc_scales, bc, W1_words, W1_scales, b1, o
         regroup(1, nc.scalar.copy)
         halve(0, 1)
         permute_planes(0)
+        quantise_pass(0, 0)
         halve(0, 2)
-        halve(1, 1)
-        quantise(0)
-        permute_words(0, 0)
+        permute_words_pass(0, 0, 0)
+        quantise_pass(0, 1)
+        permute_words_pass(0, 0, 1)
         means(0)
-        halve(0, 3)
+        halve(1, 1)
         add_eps(0, 0, 1)
         permute_words(0, 1)
         take_inverse(0, 0, 1)
-        halve(1, 2)
+        halve(0, 3)
         scale_bias(0, 0, 1)
+        halve(1, 2)
         whole_half(0, 0, 0, (S, S))
         whole_half(0, 0, 1, (S, S))
         quantise(1)
@@ -320,14 +335,13 @@ def tile_wb_pa_kernel(tc, x, Wc_words, Wc_scales, bc, W1_words, W1_scales, b1, o
         top_maximum(1)
         scale_bias(0, 1, 1)
         whole_half(1, 0, 0, (S, S))
-        add_eps(1, 0, 2)
-        regroup(2, nc.vector.tensor_copy)
         permute_planes(1)
-        take_inverse(1, 0, 2)
+        add_eps(1, 0, 2)
         permute_words(1, 0)
+        take_inverse(1, 0, 2)
+        regroup(2, nc.vector.tensor_copy)
         scale_bias(1, 0, 2)
         whole_half(1, 0, 1, (S, S))
-        add_pixels(2)
         permute_words(1, 1)
         whole_half(0, 1, 0, (S, S))
         halve(2, 1)
@@ -337,44 +351,45 @@ def tile_wb_pa_kernel(tc, x, Wc_words, Wc_scales, bc, W1_words, W1_scales, b1, o
         regroup_pass(3, 0, nc.vector.tensor_copy)
         halve(2, 3)
         whole_half(0, 1, 1, (S, S))
-        means(2)
         halve(3, 1)
-        add_eps(0, 2, 1)
         top_maximum(2)
-        take_inverse(0, 2, 1)
         regroup_pass(3, 1, nc.vector.tensor_copy)
-        scale_bias(0, 2, 1)
         add_eps(1, 2, 1)
         whole_half(1, 1, 1, (S, S))
         halve(3, 2)
         take_inverse(1, 2, 1)
         quantise(3)
         scale_bias(1, 2, 1)
-        whole_half(2, 0, 0, (S, S))
+        whole_half(2, 1, 0, (S, S))
+        sum_on_vector(2)
         halve(3, 3)
-        whole_half(2, 0, 1, (S, S))
-        sum_on_vector(3)
+        whole_half(2, 1, 1, (S, S))
+        mean_divisor(2)
         top_maximum(3)
-        mean_divisor(3)
-        fill(2, 1, 0, 2)
-        empty(2, 1, 0, V)
+        take_inverse(0, 2, 1)
         add_eps(1, 3, 1)
-        take_inverse(0, 3, 1)
-        empty(2, 1, 1, V)
-        store(2, 1, 0, 2)
+        fill(2, 0, 0, 2)
+        scale_bias(0, 2, 1)
+        empty(2, 0, 0, S)
+        empty(2, 0, 1, S)
+        store(2, 0, 0, 2)
         take_inverse(1, 3, 1)
-        scale_bias(0, 3, 1)
-        fill(2, 1, 2, 2)
-        empty(2, 1, 2, V)
+        sum_on_vector(3)
         scale_bias(1, 3, 1)
-        empty(2, 1, 3, V)
-        store(2, 1, 2, 2)
-        half(2, 1, 1, (S, S))
-        half(3, 0, 0, (S, V))
-        half(3, 0, 1, (S, V))
-        half(3, 1, 0, (S, V))
-        fill_and_empty(3, 1, 4, 2, S)
-        store(3, 1, 4, 2)
-        fill_and_empty(3, 1, 6, 1, V)
-        fill_and_empty(3, 1, 7, 1, S)
-        store(3, 1, 6, 2)
+        bank(2, 0, 0, 1, S)
+        half(2, 0, 1, (S, S))
+        mean_divisor(3)
+        bank(3, 1, 0, 0, S)
+        fill(3, 1, 2, 2)
+        empty(3, 1, 2, V)
+        take_inverse(0, 3, 1)
+        empty(3, 1, 3, V)
+        store(3, 1, 2, 2)
+        scale_bias(0, 3, 1)
+        half(3, 1, 1, (S, V))
+        half(3, 0, 0, (V, S))
+        fill_and_empty(3, 0, 4, 2, V)
+        store(3, 0, 4, 2)
+        fill_and_empty(3, 0, 6, 1, V)
+        fill_and_empty(3, 0, 7, 1, S)
+        store(3, 0, 6, 2)

@@ -184,6 +184,25 @@ def tile_wb_pa_kernel(tc, x, Wc_words, Wc_scales, bc, W1_words, W1_scales, b1, o
         def sum_on_vector(b):
             nc.vector.tensor_reduce(out=stat[:, 0, b, :], in_=x_sb[b][:], axis=AX.X, op=ALU.add)
 
+        def add_last_pass(b):
+            wide = 2 * SUM_CHUNK
+            sums[b] = psum.tile([P, PACK, wide], F32, name="sums", tag="bank")
+            chunks = PIXELS // wide
+            for c in range(chunks):
+                nc.tensor.matmul(
+                    out=sums[b][:],
+                    lhsT=ident[:],
+                    rhs=x_sb[b][:, PACK : 2 * PACK, wide * c : wide * (c + 1)],
+                    start=(c == 0),
+                    stop=(c == chunks - 1),
+                )
+
+        def sum_first_pass(b):
+            nc.vector.tensor_reduce(out=stat[:, 0, b, 0:PACK], in_=x_sb[b][:, 0:PACK, :], axis=AX.X, op=ALU.add)
+
+        def sum_last_pass(b):
+            nc.vector.tensor_reduce(out=stat[:, 0, b, PACK : 2 * PACK], in_=sums[b][:], axis=AX.X, op=ALU.add)
+
         def mean_divisor(b):
             nc.vector.tensor_scalar(
                 out=divisor[:, 0, b],
@@ -355,13 +374,15 @@ def tile_wb_pa_kernel(tc, x, Wc_words, Wc_scales, bc, W1_words, W1_scales, b1, o
         top_maximum(2)
         regroup_pass(3, 1, nc.vector.tensor_copy)
         add_eps(1, 2, 1)
+        add_last_pass(2)
         whole_half(1, 1, 1, (S, S))
         halve(3, 2)
         take_inverse(1, 2, 1)
         quantise(3)
         scale_bias(1, 2, 1)
         whole_half(2, 1, 0, (S, S))
-        sum_on_vector(2)
+        sum_first_pass(2)
+        sum_last_pass(2)
         halve(3, 3)
         whole_half(2, 1, 1, (S, S))
         mean_divisor(2)
@@ -386,8 +407,8 @@ def tile_wb_pa_kernel(tc, x, Wc_words, Wc_scales, bc, W1_words, W1_scales, b1, o
         empty(3, 1, 3, V)
         store(3, 1, 2, 2)
         scale_bias(0, 3, 1)
-        half(3, 1, 1, (S, V))
-        half(3, 0, 0, (V, S))
+        whole_half(3, 1, 1, (S, V))
+        whole_half(3, 0, 0, (V, S))
         fill_and_empty(3, 0, 4, 2, V)
         store(3, 0, 4, 2)
         fill_and_empty(3, 0, 6, 1, V)

@@ -111,9 +111,9 @@ def tile_wb_pa_kernel(tc, x, Wc_words, Wc_scales, bc, W1_words, W1_scales, b1, o
         load_words(0, 1)
         load_bias(0)
         load_image(2)
-        load_bias(1)
         load_scales(1)
         load_words(1, 0)
+        load_bias(1)
         load_words(1, 1)
         load_image(3)
 
@@ -381,8 +381,8 @@ def tile_wb_pa_kernel(tc, x, Wc_words, Wc_scales, bc, W1_words, W1_scales, b1, o
         quantise(3)
         scale_bias(1, 2, 1)
         whole_half(2, 1, 0, (S, S))
-        sum_first_pass(2)
         sum_last_pass(2)
+        sum_first_pass(2)
         halve(3, 3)
         whole_half(2, 1, 1, (S, S))
         mean_divisor(2)
@@ -400,12 +400,12 @@ def tile_wb_pa_kernel(tc, x, Wc_words, Wc_scales, bc, W1_words, W1_scales, b1, o
         bank(2, 0, 0, 1, S)
         half(2, 0, 1, (S, S))
         mean_divisor(3)
-        bank(3, 1, 0, 0, S)
+        fill_and_empty(3, 1, 0, 2, S)
         fill(3, 1, 2, 2)
         empty(3, 1, 2, V)
         take_inverse(0, 3, 1)
         empty(3, 1, 3, V)
-        store(3, 1, 2, 2)
+        store(3, 1, 0, 4)
         scale_bias(0, 3, 1)
         whole_half(3, 1, 1, (S, V))
         whole_half(3, 0, 0, (V, S))

from contextlib import ExitStack

import concourse.mybir as mybir
from concourse.masks import make_identity

F32 = mybir.dt.float32
BF16 = mybir.dt.bfloat16
I32 = mybir.dt.int32
U32 = mybir.dt.uint32
U8 = mybir.dt.uint8
FP8X4 = mybir.dt.float8_e4m3fn_x4
ALU = mybir.AluOpType
ACT = mybir.ActivationFunctionType
AX = mybir.AxisListType

IMAGES = 4
CHANNELS = 1024
PIXELS = 256
EPS = 1e-05

P = 128
PACK = 4
K_PASS = P * PACK
PASSES = CHANNELS // K_PASS
HALVES = CHANNELS // K_PASS
ROWS = PASSES * PACK
O_TILES = HALVES * PACK
QUADRANTS = 4
IN_QUADRANT = P // QUADRANTS
SUM_CHUNK = 16
BANK_TILES = 2
BIAS_ROW = 16
MAX_HALVINGS = 3

FLOPS = 2 * 2 * CHANNELS * CHANNELS * IMAGES * PIXELS


def tile_wb_pa_kernel(tc, x, Wc_words, Wc_scales, bc, W1_words, W1_scales, b1, out_0, out_1):
    nc = tc.nc
    words_in = (Wc_words, W1_words)
    scales_in = (Wc_scales, W1_scales)
    bias_in = (bc, b1)
    outs = (out_0, out_1)

    with ExitStack() as ctx:
        ctx.enter_context(tc.manual_schedule())
        const = ctx.enter_context(tc.tile_pool(name="const", bufs=1))
        image = ctx.enter_context(tc.tile_pool(name="image", bufs=1))
        result = ctx.enter_context(tc.tile_pool(name="result", bufs=1))
        psum = ctx.enter_context(tc.psum_pool(name="psum", bufs=8))

        planes_in = []
        for w in range(2):
            planes_w = const.tile([P, CHANNELS], U8, name="planes_in%d" % w)
            nc.vector.memset(planes_w[:].bitcast(I32), 0)
            planes_in.append(planes_w)
        warm = const.tile([P, 2], F32)
        nc.vector.memset(warm[:], 0.0)
        nc.scalar.activation(out=warm[:, 1:2], in_=warm[:, 0:1], func=ACT.Identity)
        ident = const.tile([P, P], BF16)
        nc.vector.memset(ident[:], 0.0)
        make_identity(nc, ident[:], nomemset=True)

        x_sb = []

        def load_image(b, pieces=1):
            x_b = image.tile([P, ROWS, PIXELS], BF16, name="x%d" % b)
            width = PASSES // pieces
            for g in range(0, PASSES, width):
                nc.sync.dma_start(
                    out=x_b[:, PACK * g : PACK * (g + width), :].rearrange("p (g t) n -> p g (t n)", g=width),
                    in_=x[b].rearrange("(g p t) h w -> p g (t h w)", g=PASSES, p=P, t=PACK)[:, g : g + width],
                )
            x_sb.append(x_b)

        def load_scales(w):
            for quadrant in range(QUADRANTS):
                first = IN_QUADRANT * quadrant
                nc.sync.dma_start(
                    out=planes_in[w][first : first + PACK * PASSES, :].bitcast(I32),
                    in_=scales_in[w][:, PACK * quadrant : PACK * (quadrant + 1), :].bitcast(I32),
                )

        bias_bf = const.tile([P, 2, BIAS_ROW], BF16)

        def load_bias(w):
            nc.sync.dma_start(
                out=bias_bf[:, w, 0:O_TILES].rearrange("p (h t) -> p h t", h=HALVES),
                in_=bias_in[w].rearrange("(h p t) -> p h t", h=HALVES, p=P, t=PACK),
            )

        words_sb = [const.tile([P, HALVES, PASSES, K_PASS], I32, name="words_in%d" % w) for w in range(2)]

        def load_words(w, h):
            nc.sync.dma_start(
                out=words_sb[w][:, h],
                in_=words_in[w][:, :, K_PASS * h : K_PASS * (h + 1), :].rearrange("g p n t -> p g (n t)").bitcast(I32),
            )

        def load_words_pass(w, h, g):
            nc.sync.dma_start(
                out=words_sb[w][:, h, g],
                in_=words_in[w][g, :, K_PASS * h : K_PASS * (h + 1), :].rearrange("p n t -> p (n t)").bitcast(I32),
            )

        load_image(0, 2)
        load_scales(0)
        load_image(1)
        load_words_pass(0, 0, 0)
        load_words_pass(0, 0, 1)
        load_words(0, 1)
        load_bias(0)
        load_image(2)
        load_scales(1)
        load_words(1, 0)
        load_bias(1)
        load_words(1, 1)
        load_image(3)

        averager = const.tile([P, P], BF16)
        nc.vector.tensor_scalar(out=averager[:], in0=ident[:], scalar1=1.0 / PIXELS, scalar2=None, op0=ALU.mult)

        w_planes = [const.tile([P, CHANNELS], U8, name="w_planes%d" % w, align_bytes=64) for w in range(2)]
        w_words = [
            const.tile([P, HALVES, PASSES, PACK, P], I32, name="w_words%d" % w, align_bytes=64) for w in range(2)
        ]

        stat = const.tile([P, 2, IMAGES, ROWS], F32)
        x_codes = const.tile([P, IMAGES, PASSES, PIXELS], U32, align_bytes=64)
        x_planes = const.tile([P, IMAGES, PASSES, PIXELS], U8, align_bytes=64)
        divisor = const.tile([P, 2, IMAGES, O_TILES], F32)
        inverse = const.tile([P, 2, IMAGES, O_TILES], F32)
        offset = const.tile([P, 2, IMAGES, O_TILES], F32)

        grouped = {}
        narrowed = {}
        sums = {}

        def permute_planes(w):
            nc.vector.tensor_copy(
                out=w_planes[w][:].rearrange("p (h t m) -> p h m t", h=HALVES, t=PACK),
                in_=planes_in[w][:].rearrange("p (h m t) -> p h m t", h=HALVES, t=PACK),
            )

        def permute_words(w, h):
            nc.vector.tensor_copy(
                out=w_words[w][:, h].rearrange("p g t m -> p g m t"),
                in_=words_sb[w][:, h].rearrange("p g (m t) -> p g m t", t=PACK),
            )

        def permute_words_pass(w, h, g):
            nc.vector.tensor_copy(
                out=w_words[w][:, h, g].rearrange("p t m -> p m t"),
                in_=words_sb[w][:, h, g].rearrange("p (m t) -> p m t", t=PACK),
            )

        def add_pixels(b):
            sums[b] = psum.tile([P, ROWS, SUM_CHUNK], F32, name="sums", tag="bank")
            chunks = PIXELS // SUM_CHUNK
            for c in range(chunks):
                nc.tensor.matmul(
                    out=sums[b][:],
                    lhsT=averager[:],
                    rhs=x_sb[b][:, :, SUM_CHUNK * c : SUM_CHUNK * (c + 1)],
                    start=(c == 0),
                    stop=(c == chunks - 1),
                )

        def halve(b, halving):
            widest = x_sb[b] if halving == 1 else narrowed[b]
            width = PIXELS >> halving
            narrower = image.tile([P, ROWS, width], BF16, name="max%d_%d" % (b, width))
            nc.vector.tensor_tensor(
                out=narrower[:], in0=widest[:, :, 0:width], in1=widest[:, :, width : 2 * width], op=ALU.max
            )
            narrowed[b] = narrower

        def top_maximum(b):
            nc.vector.tensor_reduce(out=stat[:, 1, b, :], in_=narrowed[b][:], axis=AX.X, op=ALU.max)

        def means(b):
            nc.vector.tensor_reduce(out=stat[:, 0, b, :], in_=sums[b][:], axis=AX.X, op=ALU.add)

        def sum_on_vector(b):
            nc.vector.tensor_reduce(out=stat[:, 0, b, :], in_=x_sb[b][:], axis=AX.X, op=ALU.add)

        def add_last_pass(b):
            wide = 2 * SUM_CHUNK
            sums[b] = psum.tile([P, PACK, wide], F32, name="sums", tag="bank")
            chunks = PIXELS // wide
            for c in range(chunks):
                nc.tensor.matmul(
                    out=sums[b][:],
                    lhsT=ident[:],
                    rhs=x_sb[b][:, PACK : 2 * PACK, wide * c : wide * (c + 1)],
                    start=(c == 0),
                    stop=(c == chunks - 1),
                )

        def sum_first_pass(b):
            nc.vector.tensor_reduce(out=stat[:, 0, b, 0:PACK], in_=x_sb[b][:, 0:PACK, :], axis=AX.X, op=ALU.add)

        def sum_last_pass(b):
            nc.vector.tensor_reduce(out=stat[:, 0, b, PACK : 2 * PACK], in_=sums[b][:], axis=AX.X, op=ALU.add)

        def mean_divisor(b):
            nc.vector.tensor_scalar(
                out=divisor[:, 0, b],
                in0=stat[:, 0, b, :],
                scalar1=1.0 / PIXELS,
                scalar2=EPS,
                op0=ALU.mult,
                op1=ALU.add,
            )

        def regroup_pass(b, g, copy):
            if b not in grouped:
                grouped[b] = image.tile([P, PASSES, PIXELS, PACK], BF16, name="grouped%d" % b, align_bytes=64)
            copy(
                out=grouped[b][:, g].rearrange("p (c i) t -> p c t i", i=4),
                in_=x_sb[b][:, PACK * g : PACK * (g + 1), :].rearrange("p t (c i) -> p c t i", i=4),
            )

        def regroup(b, copy):
            for g in range(PASSES):
                regroup_pass(b, g, copy)

        def quantise(b):
            nc.vector.quantize_mx(
                out=x_codes[:, b].rearrange("p g n -> p (g n)").bitcast(FP8X4),
                scales=x_planes[:, b].rearrange("p g n -> p (g n)"),
                in_=grouped[b][:].rearrange("p g n t -> p (g n t)"),
            )

        def quantise_pass(b, g):
            nc.vector.quantize_mx(
                out=x_codes[:, b, g].bitcast(FP8X4),
                scales=x_planes[:, b, g],
                in_=grouped[b][:, g].rearrange("p n t -> p (n t)"),
            )

        def add_eps(w, first, count):
            images = slice(first, first + count)
            nc.vector.tensor_scalar(
                out=divisor[:, w, images], in0=stat[:, w, images], scalar1=EPS, scalar2=None, op0=ALU.add
            )

        def take_inverse(w, first, count):
            images = slice(first, first + count)
            nc.vector.reciprocal(out=inverse[:, w, images], in_=divisor[:, w, images])

        def scale_bias(w, first, count):
            images = slice(first, first + count)
            nc.vector.tensor_tensor(
                out=offset[:, w, images],
                in0=bias_bf[:, w : w + 1, 0:O_TILES].to_broadcast([P, count, O_TILES]),
                in1=inverse[:, w, images],
                op=ALU.mult,
            )

        y_sb = {}
        products = {}

        def fill_and_empty(b, w, first, count, engine):
            fill(b, w, first, count)
            for i in range(count):
                empty(b, w, first + i, engine)

        def fill(b, w, first, count):
            if (b, w) not in y_sb:
                y_sb[(b, w)] = result.tile([P, O_TILES, PIXELS], F32, name="y%d_%d" % (b, w))
            acc = psum.tile([P, BANK_TILES, PIXELS], F32, name="acc", tag="bank")
            for i in range(count):
                products[(b, w, first + i)] = acc[:, i, :]
                h, t = divmod(first + i, PACK)
                for g in range(PASSES):
                    nc.tensor.matmul_mx(
                        out=acc[:, i, :],
                        lhsT=w_words[w][:, h, g, t, :].bitcast(FP8X4),
                        lhsT_scale=w_planes[w][PACK * g : P, K_PASS * h + P * t : K_PASS * h + P * (t + 1)],
                        rhs=x_codes[:, b, g, :].bitcast(FP8X4),
                        rhs_scale=x_planes[:, b, g, :],
                        start=(g == 0),
                        stop=(g == PASSES - 1),
                    )

        def empty(b, w, j, engine):
            y = y_sb[(b, w)]
            if engine == "vector":
                nc.vector.tensor_scalar(
                    out=y[:, j, :],
                    in0=products[(b, w, j)],
                    scalar1=inverse[:, w, b, j : j + 1],
                    scalar2=offset[:, w, b, j : j + 1],
                    op0=ALU.mult,
                    op1=ALU.add,
                )
            else:
                nc.scalar.activation(
                    out=y[:, j, :],
                    in_=products[(b, w, j)],
                    func=ACT.Identity,
                    bias=offset[:, w, b, j : j + 1],
                    scale=inverse[:, w, b, j : j + 1],
                )

        def store(b, w, first, count):
            h, t = divmod(first, PACK)
            out_view = outs[w][b].rearrange("(h p t) r c -> p h t (r c)", h=HALVES, p=P, t=PACK)
            nc.sync.dma_start(out=out_view[:, h, t : t + count, :], in_=y_sb[(b, w)][:, first : first + count, :])

        def bank(b, w, h, i, engine):
            fill_and_empty(b, w, PACK * h + BANK_TILES * i, BANK_TILES, engine)
            store(b, w, PACK * h + BANK_TILES * i, BANK_TILES)

        def half(b, w, h, engines):
            for i, engine in enumerate(engines):
                bank(b, w, h, i, engine)

        def whole_half(b, w, h, engines):
            for i, engine in enumerate(engines):
                fill_and_empty(b, w, PACK * h + BANK_TILES * i, BANK_TILES, engine)
            store(b, w, PACK * h, PACK)

        S, V = "scalar", "vector"

        add_pixels(0)
        add_pixels(1)
        regroup(0, nc.scalar.copy)
        regroup(1, nc.scalar.copy)
        halve(0, 1)
        permute_planes(0)
        quantise_pass(0, 0)
        halve(0, 2)
        permute_words_pass(0, 0, 0)
        quantise_pass(0, 1)
        permute_words_pass(0, 0, 1)
        means(0)
        halve(1, 1)
        add_eps(0, 0, 1)
        permute_words(0, 1)
        take_inverse(0, 0, 1)
        halve(0, 3)
        scale_bias(0, 0, 1)
        halve(1, 2)
        whole_half(0, 0, 0, (S, S))
        whole_half(0, 0, 1, (S, S))
        quantise(1)
        means(1)
        halve(1, 3)
        add_eps(0, 1, 1)
        top_maximum(0)
        take_inverse(0, 1, 1)
        top_maximum(1)
        scale_bias(0, 1, 1)
        whole_half(1, 0, 0, (S, S))
        permute_planes(1)
        add_eps(1, 0, 2)
        permute_words(1, 0)
        take_inverse(1, 0, 2)
        regroup(2, nc.vector.tensor_copy)
        scale_bias(1, 0, 2)
        whole_half(1, 0, 1, (S, S))
        permute_words(1, 1)
        whole_half(0, 1, 0, (S, S))
        halve(2, 1)
        quantise(2)
        whole_half(1, 1, 0, (S, S))
        halve(2, 2)
        regroup_pass(3, 0, nc.vector.tensor_copy)
        halve(2, 3)
        whole_half(0, 1, 1, (S, S))
        halve(3, 1)
        top_maximum(2)
        regroup_pass(3, 1, nc.vector.tensor_copy)
        add_eps(1, 2, 1)
        add_last_pass(2)
        whole_half(1, 1, 1, (S, S))
        halve(3, 2)
        take_inverse(1, 2, 1)
        quantise(3)
        scale_bias(1, 2, 1)
        whole_half(2, 1, 0, (S, S))
        sum_last_pass(2)
        sum_first_pass(2)
        halve(3, 3)
        whole_half(2, 1, 1, (S, S))
        mean_divisor(2)
        top_maximum(3)
        take_inverse(0, 2, 1)
        add_eps(1, 3, 1)
        fill(2, 0, 0, 2)
        scale_bias(0, 2, 1)
        empty(2, 0, 0, S)
        empty(2, 0, 1, S)
        store(2, 0, 0, 2)
        take_inverse(1, 3, 1)
        sum_on_vector(3)
        scale_bias(1, 3, 1)
        bank(2, 0, 0, 1, S)
        half(2, 0, 1, (S, S))
        mean_divisor(3)
        fill_and_empty(3, 1, 0, 2, S)
        fill(3, 1, 2, 2)
        empty(3, 1, 2, V)
        take_inverse(0, 3, 1)
        empty(3, 1, 3, V)
        store(3, 1, 0, 4)
        scale_bias(0, 3, 1)
        whole_half(3, 1, 1, (S, V))
        whole_half(3, 0, 0, (V, S))
        fill_and_empty(3, 0, 4, 2, V)
        store(3, 0, 4, 2)
        fill_and_empty(3, 0, 6, 1, V)
        fill_and_empty(3, 0, 7, 1, S)
        store(3, 0, 6, 2)
